import numpy as np
import ml_dtypes


def mxq(x, axis, fmt="e4m3"):
    dtype, down = {"e4m3": (ml_dtypes.float8_e4m3fn, 7), "e5m2": (ml_dtypes.float8_e5m2, 14)}[fmt]
    v = np.moveaxis(np.asarray(x, np.float32).astype(ml_dtypes.bfloat16).astype(np.float64), axis, -1)
    blocks = v.reshape(v.shape[:-1] + (-1, 32))
    amax = np.abs(blocks).max(-1, keepdims=True)
    byte = np.maximum(np.where(amax > 0, np.frexp(amax)[1] - 1 + 127, 0) - down, 1)
    scale = np.exp2(byte - 127.0)
    codes = (blocks / scale).astype(np.float32).astype(dtype).astype(np.float64)
    return np.moveaxis((codes * scale).reshape(v.shape), -1, axis)


WIDE = False


def mx_kscale(k):
    if not WIDE:
        return np.ones(k)
    levels = np.array([10, -10, 5, -5, 0])
    a = np.random.permutation(np.resize(levels, k // 512 * 4)).reshape(k // 512, 4)
    idx = np.arange(k)
    return np.exp2(a[idx // 512, idx % 128 // 32])


BF16 = ml_dtypes.bfloat16


def bf(x):
    return np.asarray(x, np.float32).astype(BF16)


def f64(x):
    return np.asarray(x).astype(np.float64)


B, PED, NED, CED = 1536, 320, 128, 512
Q = PED // 4
FEAT = 2 * PED + 3 * NED


def leaky(v):
    return np.where(v >= 0.0, v, 0.01 * v)


def point_enc(xy, wsx, bsx, wcx, bcx, wsy, bsy, wcy, bcy):
    x = xy[:, 0:1]
    y = xy[:, 1:2]
    return np.concatenate([np.sin(x * wsx + bsx), np.cos(x * wcx + bcx), np.sin(y * wsy + bsy), np.cos(y * wcy + bcy)], axis=-1)


def num_enc(t, w, b):
    return leaky(t[:, None] * w + b)


def setup_inputs():
    s = np.array(mx_kscale(FEAT), dtype=np.float64)
    s[:2 * PED] = 1.0
    t = mx_kscale(CED)
    d = {'src_xy': bf(np.random.standard_normal((B, 2))), 'dst_xy': bf(np.random.standard_normal((B, 2))),
         'time_s': bf(np.random.uniform(size=B)), 'wait_src': bf(np.random.uniform(size=B)), 'wait_dst': bf(np.random.uniform(size=B))}
    for pfx in ('src', 'dst'):
        for part in ('wsx', 'bsx', 'wcx', 'bcx', 'wsy', 'bsy', 'wcy', 'bcy'):
            d[pfx + '_' + part] = bf(np.random.standard_normal(Q) * (1.0 if part[0] == 'w' else 0.1))
    for i, pfx in enumerate(('t', 'ws', 'wd')):
        sn = s[2 * PED + i * NED:2 * PED + (i + 1) * NED]
        d[pfx + '_w'] = bf(np.random.standard_normal(NED) * sn)
        d[pfx + '_b'] = bf(np.random.standard_normal(NED) * 0.1 * sn)
    d['W1'] = bf(np.random.standard_normal((FEAT, CED)) * 1.5 / np.sqrt(FEAT) / s[:, None] * t[None, :])
    d['b1'] = bf(np.random.standard_normal(CED) * 0.1 * t)
    d['W2'] = bf(np.random.standard_normal((CED, CED)) * 1.5 / np.sqrt(CED) / t[:, None])
    d['b2'] = bf(np.random.standard_normal(CED) * 0.1)
    return d


def reference(src_xy, dst_xy, time_s, wait_src, wait_dst,
              src_wsx, src_bsx, src_wcx, src_bcx, src_wsy, src_bsy, src_wcy, src_bcy,
              dst_wsx, dst_bsx, dst_wcx, dst_bcx, dst_wsy, dst_bsy, dst_wcy, dst_bcy,
              t_w, t_b, ws_w, ws_b, wd_w, wd_b,
              W1, b1, W2, b2):
    feats = np.concatenate([
        point_enc(f64(src_xy), f64(src_wsx), f64(src_bsx), f64(src_wcx), f64(src_bcx),
                        f64(src_wsy), f64(src_bsy), f64(src_wcy), f64(src_bcy)),
        point_enc(f64(dst_xy), f64(dst_wsx), f64(dst_bsx), f64(dst_wcx), f64(dst_bcx),
                        f64(dst_wsy), f64(dst_bsy), f64(dst_wcy), f64(dst_bcy)),
        num_enc(f64(time_s), f64(t_w), f64(t_b)),
        num_enc(f64(wait_src), f64(ws_w), f64(ws_b)),
        num_enc(f64(wait_dst), f64(wd_w), f64(wd_b)),
    ], axis=-1)
    h = leaky((mxq(feats, 1, 'e4m3') @ mxq(f64(W1), 0, 'e4m3')) + f64(b1))
    return leaky((mxq(h, 1, 'e4m3') @ mxq(f64(W2), 0, 'e4m3')) + f64(b2))

@@ -1,0 +1,256 @@
+import math
+from contextlib import ExitStack
+
+import concourse.mybir as mybir
+
+F32 = mybir.dt.float32
+BF16 = mybir.dt.bfloat16
+I32 = mybir.dt.int32
+U32 = mybir.dt.uint32
+U8 = mybir.dt.uint8
+FP8X4 = mybir.dt.float8_e4m3fn_x4
+ALU = mybir.AluOpType
+ACT = mybir.ActivationFunctionType
+
+P = 128
+B = 1536
+CH = 512
+NCH = B // CH
+H = 512
+SLOTS = 5
+TWO_PI = 2.0 * math.pi
+SLOPE = 0.01
+
+FLOPS = 2 * B * 1024 * H + 2 * B * H * H
+
+
+def row(vec):
+    return vec.rearrange("(o n) -> o n", o=1)
+
+
+def regroup(copy, dst, src):
+    copy(
+        out=dst.rearrange("p (c i) t -> p c t i", i=4),
+        in_=src.rearrange("p t (c i) -> p c t i", i=4),
+    )
+
+
+def tile_claimencoder_kernel(
+    tc,
+    src_xy, dst_xy, time_s, wait_src, wait_dst,
+    src_wsx, src_bsx, src_wcx, src_bcx, src_wsy, src_bsy, src_wcy, src_bcy,
+    dst_wsx, dst_bsx, dst_wcx, dst_bcx, dst_wsy, dst_bsy, dst_wcy, dst_bcy,
+    t_w, t_b, ws_w, ws_b, wd_w, wd_b,
+    W1, b1, W2, b2,
+    out,
+):
+    nc = tc.nc
+    with ExitStack() as ctx:
+        keep = ctx.enter_context(tc.tile_pool(name="keep", bufs=1))
+        work = ctx.enter_context(tc.tile_pool(name="work", bufs=2))
+        ps1 = ctx.enter_context(tc.psum_pool(name="ps1", bufs=4))
+        ps2 = ctx.enter_context(tc.psum_pool(name="ps2", bufs=2))
+        ps3 = ctx.enter_context(tc.psum_pool(name="ps3", bufs=2))
+
+        w1s = keep.tile([P, SLOTS, H], BF16)
+        nc.sync.dma_start(out=w1s[:], in_=W1[0:640, :].rearrange("(p s) n -> p s n", s=SLOTS))
+        w1n = keep.tile([P, 3, H], BF16)
+        nc.sync.dma_start(out=w1n[:], in_=W1[640:1024, :].rearrange("(t p) n -> p t n", p=P))
+
+        num_wb = keep.tile([P, 3, P], BF16)
+        nc.vector.memset(num_wb[:], 0.0)
+        rows_num = keep.tile([P, B], BF16)
+        nc.vector.memset(rows_num[:], 0.0)
+        nc.vector.memset(rows_num[96:128, :], 1.0)
+        for t, (scal, w_t, b_t) in enumerate(((time_s, t_w, t_b), (wait_src, ws_w, ws_b), (wait_dst, wd_w, wd_b))):
+            nc.scalar.dma_start(out=num_wb[32 * t : 32 * t + 1, t, :], in_=row(w_t))
+            nc.scalar.dma_start(out=num_wb[96:97, t, :], in_=row(b_t))
+            nc.scalar.dma_start(out=rows_num[32 * t : 32 * t + 1, :], in_=row(scal))
+
+        pw = keep.tile([P, SLOTS], BF16)
+        pb = keep.tile([P, SLOTS], BF16)
+        groups = (
+            (src_wsx, src_bsx, src_wcx, src_bcx),
+            (src_wsy, src_bsy, src_wcy, src_bcy),
+            (dst_wsx, dst_bsx, dst_wcx, dst_bcx),
+            (dst_wsy, dst_bsy, dst_wcy, dst_bcy),
+        )
+        for g, (w_sin, b_sin, w_cos, b_cos) in enumerate(groups):
+            lo = 32 * g
+            nc.sync.dma_start(out=pw[lo : lo + 16, :], in_=w_sin.rearrange("(l s) -> l s", s=SLOTS))
+            nc.sync.dma_start(out=pw[lo + 16 : lo + 32, :], in_=w_cos.rearrange("(l s) -> l s", s=SLOTS))
+            nc.gpsimd.dma_start(out=pb[lo : lo + 16, :], in_=b_sin.rearrange("(l s) -> l s", s=SLOTS))
+            nc.gpsimd.dma_start(out=pb[lo + 16 : lo + 32, :], in_=b_cos.rearrange("(l s) -> l s", s=SLOTS))
+
+        rows_xy = keep.tile([P, 2 * B], BF16)
+        nc.vector.memset(rows_xy[:], 0.0)
+        flat_s = src_xy.rearrange("b c -> (b c)")
+        flat_d = dst_xy.rearrange("b c -> (b c)")
+        nc.scalar.dma_start(out=rows_xy[0:1, :], in_=row(flat_s))
+        nc.scalar.dma_start(out=rows_xy[32:33, 0 : 2 * B - 1], in_=row(flat_s[1 : 2 * B]))
+        nc.scalar.dma_start(out=rows_xy[64:65, :], in_=row(flat_d))
+        nc.scalar.dma_start(out=rows_xy[96:97, 0 : 2 * B - 1], in_=row(flat_d[1 : 2 * B]))
+
+        w2 = keep.tile([P, 4, H], BF16)
+        nc.sync.dma_start(out=w2[:], in_=W2.rearrange("(t p) n -> p t n", p=P))
+        b1raw = keep.tile([P, 4], BF16)
+        with nc.allow_non_contiguous_dma(reason="512 bias values, one per partition and output tile"):
+            nc.sync.dma_start(out=b1raw[:], in_=b1.rearrange("(m p) -> p m", p=P))
+        b2bc = keep.tile([P, H], BF16)
+        nc.sync.dma_start(out=b2bc[:], in_=b2.partition_broadcast(P))
+
+        sel = keep.tile([P, P], BF16)
+        nc.vector.memset(sel[:], 0.0)
+        for g in range(4):
+            nc.vector.memset(sel[32 * g : 32 * g + 32, 32 * g : 32 * g + 32], 1.0)
+
+        g_b = keep.tile([P, CH, 4], BF16, align_bytes=64)
+        g_c = keep.tile([P, CH, 4], BF16, align_bytes=64)
+        nc.gpsimd.memset(g_c[:].rearrange("p n t -> p (n t)").bitcast(F32), 0.0)
+        nc.gpsimd.memset(g_b[:].rearrange("p n t -> p (n t)").bitcast(F32), 0.0)
+
+        lane = keep.tile([P, 1], I32)
+        nc.gpsimd.iota(lane[:], pattern=[[0, 1]], base=0, channel_multiplier=1)
+        bit = keep.tile([P, 1], I32)
+        nc.vector.tensor_scalar(out=bit[:], in0=lane[:], scalar1=16, scalar2=None, op0=ALU.bitwise_and)
+        phase = keep.tile([P, 1], F32)
+        nc.vector.tensor_scalar(out=phase[:], in0=bit[:], scalar1=math.pi / 32.0, scalar2=None, op0=ALU.mult)
+        wq = keep.tile([P, SLOTS], F32)
+        nc.vector.tensor_scalar(out=wq[:], in0=pw[:], scalar1=1.0 / TWO_PI, scalar2=None, op0=ALU.mult)
+        sb = keep.tile([P, SLOTS], F32)
+        nc.vector.tensor_scalar(out=sb[:], in0=pb[:], scalar1=phase[:, 0:1], scalar2=None, op0=ALU.add)
+        bq = keep.tile([P, SLOTS], F32)
+        nc.vector.tensor_scalar(out=bq[:], in0=sb[:], scalar1=1.0 / TWO_PI, scalar2=None, op0=ALU.mult)
+        b1f = keep.tile([P, 4], F32)
+        nc.vector.tensor_copy(out=b1f[:], in_=b1raw[:])
+        b1s = keep.tile([P, 4], F32)
+        nc.vector.tensor_scalar(out=b1s[:], in0=b1raw[:], scalar1=SLOPE, scalar2=None, op0=ALU.mult)
+
+        cw = keep.tile([P, 4, H], U32, align_bytes=64)
+        sw = keep.tile([P, 4, H], U8, align_bytes=64)
+
+        def quantise(codes, scales, grouped):
+            nc.vector.quantize_mx(
+                out=codes.bitcast(FP8X4), scales=scales, in_=grouped.rearrange("p n t -> p (n t)")
+            )
+
+        g_w1 = work.tile([P, H, 4], BF16, tag="g_a", align_bytes=64)
+        regroup(nc.vector.tensor_copy, g_w1[:], w1s[:, 0:4, :])
+        nc.scalar.copy(out=g_b[:, :, 0], in_=w1s[:, 4, :])
+        regroup(nc.scalar.copy, g_c[:, :, 0:3], w1n[:])
+        g_w2 = work.tile([P, H, 4], BF16, tag="g_a", align_bytes=64)
+        regroup(nc.scalar.copy, g_w2[:], w2[:])
+        quantise(cw[:, 0, :], sw[:, 0, :], g_w1[:])
+        quantise(cw[:, 1, :], sw[:, 1, :], g_b[:])
+        quantise(cw[:, 2, :], sw[:, 2, :], g_c[:])
+        quantise(cw[:, 3, :], sw[:, 3, :], g_w2[:])
+
+        xs = keep.tile([P, B], BF16)
+        pairs = rows_xy[:].rearrange("p (b c) -> p b c", c=2)
+        for c in range(NCH):
+            xps = ps3.tile([P, CH], F32, tag="ps3")
+            nc.tensor.matmul(out=xps[:], lhsT=sel[:], rhs=pairs[:, c * CH : (c + 1) * CH, 0], start=True, stop=True)
+            nc.scalar.copy(out=xs[:, c * CH : (c + 1) * CH], in_=xps[:])
+
+        cf = keep.tile([P, 3, B], U32, align_bytes=64)
+        sf = keep.tile([P, 3, B], U8, align_bytes=64)
+
+        def features(c):
+            cs = slice(c * CH, (c + 1) * CH)
+            planes = work.tile([P, 4, CH], BF16, tag="planes")
+            for s in range(SLOTS):
+                turns = work.tile([P, CH], I32, tag="turns", bufs=3)
+                nc.vector.tensor_scalar(
+                    out=turns[:], in0=xs[:, cs], scalar1=wq[:, s : s + 1], scalar2=bq[:, s : s + 1],
+                    op0=ALU.mult, op1=ALU.add,
+                )
+                frac = work.tile([P, CH], F32, tag="frac", bufs=4)
+                nc.vector.scalar_tensor_tensor(
+                    out=frac[:], in0=xs[:, cs], scalar=wq[:, s : s + 1], in1=turns[:],
+                    op0=ALU.mult, op1=ALU.subtract,
+                )
+                dst = planes[:, s, :] if s < 4 else g_b[:, :, 0]
+                nc.scalar.activation(out=dst, in_=frac[:], func=ACT.Sin, bias=sb[:, s : s + 1], scale=TWO_PI)
+            g_a = work.tile([P, CH, 4], BF16, tag="g_a", align_bytes=64)
+            regroup(nc.scalar.copy, g_a[:], planes[:])
+            quantise(cf[:, 0, cs], sf[:, 0, cs], g_a[:])
+            quantise(cf[:, 1, cs], sf[:, 1, cs], g_b[:])
+
+        def num_features(c):
+            cs = slice(c * CH, (c + 1) * CH)
+            for j in range(CH // P):
+                vps = ps3.tile([P, 4, P], F32, tag="ps3")
+                lo = c * CH + j * P
+                for t in range(3):
+                    nc.tensor.matmul(
+                        out=vps[:, t, :], lhsT=num_wb[:, t, :], rhs=rows_num[:, lo : lo + P], start=True, stop=True
+                    )
+                small = work.tile([P, 3, P], F32, tag="small", bufs=3)
+                nc.scalar.activation(out=small[:], in_=vps[:, 0:3, :], func=ACT.Copy, scale=SLOPE)
+                nc.vector.tensor_tensor(
+                    out=g_c[:, j * P : (j + 1) * P, 0:3],
+                    in0=vps[:, 0:3, :].rearrange("p t b -> p b t"),
+                    in1=small[:].rearrange("p t b -> p b t"),
+                    op=ALU.max,
+                )
+            quantise(cf[:, 2, cs], sf[:, 2, cs], g_c[:])
+
+        hidden = {}
+
+        def layer1(c):
+            cs = slice(c * CH, (c + 1) * CH)
+            hp = work.tile([P, 4, CH], BF16, tag="hp")
+            up = work.tile([P, 4, CH], BF16, tag="up")
+            low = work.tile([P, 4, CH], BF16, tag="low")
+            for m in range(4):
+                ms = slice(m * P, (m + 1) * P)
+                acc = ps1.tile([P, CH], F32, tag="acc1")
+                for i in range(3):
+                    nc.tensor.matmul_mx(
+                        out=acc[:],
+                        lhsT=cw[:, i, ms].bitcast(FP8X4), lhsT_scale=sw[:, i, ms],
+                        rhs=cf[:, i, cs].bitcast(FP8X4), rhs_scale=sf[:, i, cs],
+                        start=(i == 0), stop=(i == 2),
+                    )
+                nc.scalar.activation(out=up[:, m, :], in_=acc[:], func=ACT.Identity, bias=b1f[:, m : m + 1], scale=1.0)
+                nc.scalar.activation(out=low[:, m, :], in_=acc[:], func=ACT.Identity, bias=b1s[:, m : m + 1], scale=SLOPE)
+            nc.vector.tensor_tensor(out=hp[:], in0=up[:], in1=low[:], op=ALU.max)
+            g_h = work.tile([P, CH, 4], BF16, tag="g_h", align_bytes=64)
+            regroup(nc.scalar.copy, g_h[:], hp[:])
+            ch = work.tile([P, CH], U32, tag="ch", align_bytes=64)
+            sh = work.tile([P, CH], U8, tag="sh", align_bytes=64)
+            quantise(ch[:], sh[:], g_h[:])
+            hidden[c] = (ch, sh)
+
+        def layer2(c):
+            ch, sh = hidden[c]
+            for j in range(CH // P):
+                js = slice(j * P, (j + 1) * P)
+                acc = ps2.tile([P, H], F32, tag="acc2")
+                nc.tensor.matmul_mx(
+                    out=acc[:],
+                    lhsT=ch[:, js].bitcast(FP8X4), lhsT_scale=sh[:, js],
+                    rhs=cw[:, 3, :].bitcast(FP8X4), rhs_scale=sw[:, 3, :],
+                    start=True, stop=True,
+                )
+                pre = work.tile([P, H], F32, tag="pre", bufs=3)
+                nc.vector.tensor_tensor(out=pre[:], in0=acc[:], in1=b2bc[:], op=ALU.add)
+                res = work.tile([P, H], F32, tag="res", bufs=3)
+                nc.vector.scalar_tensor_tensor(
+                    out=res[:], in0=pre[:], scalar=SLOPE, in1=pre[:], op0=ALU.mult, op1=ALU.max
+                )
+                lo = c * CH + j * P
+                nc.sync.dma_start(out=out[lo : lo + P, :], in_=res[:])
+
+        num_features(0)
+        features(0)
+        num_features(1)
+        features(1)
+        layer1(0)
+        num_features(2)
+        features(2)
+        layer2(0)
+        layer1(1)
+        layer2(1)
+        layer1(2)
+        layer2(2)

@@ -48,24 +48,45 @@ def tile_claimencoder_kernel(
     with ExitStack() as ctx:
         keep = ctx.enter_context(tc.tile_pool(name="keep", bufs=1))
         work = ctx.enter_context(tc.tile_pool(name="work", bufs=2))
-        ps1 = ctx.enter_context(tc.psum_pool(name="ps1", bufs=4))
-        ps2 = ctx.enter_context(tc.psum_pool(name="ps2", bufs=2))
-        ps3 = ctx.enter_context(tc.psum_pool(name="ps3", bufs=2))
+        psum = ctx.enter_context(tc.psum_pool(name="psum", bufs=8))
+        ctx.enter_context(tc.manual_schedule())
 
         w1s = keep.tile([P, SLOTS, H], BF16)
-        nc.sync.dma_start(out=w1s[:], in_=W1[0:640, :].rearrange("(p s) n -> p s n", s=SLOTS))
-        w1n = keep.tile([P, 3, H], BF16)
-        nc.sync.dma_start(out=w1n[:], in_=W1[640:1024, :].rearrange("(t p) n -> p t n", p=P))
+        nc.gpsimd.dma_start(out=w1s[:], in_=W1[0:640, :].rearrange("(p s) n -> p s n", s=SLOTS))
 
-        num_wb = keep.tile([P, 3, P], BF16)
-        nc.vector.memset(num_wb[:], 0.0)
+        def load(dst, src):
+            nc.sync.dma_start(out=dst, in_=src)
+
+        warm = keep.tile([P, 1], F32)
+        nc.vector.memset(warm[:], 0.0)
+        warmed = keep.tile([P, 1], F32)
+        nc.scalar.activation(out=warmed[:], in_=warm[:], func=ACT.Sin)
         rows_num = keep.tile([P, B], BF16)
         nc.vector.memset(rows_num[:], 0.0)
         nc.vector.memset(rows_num[96:128, :], 1.0)
-        for t, (scal, w_t, b_t) in enumerate(((time_s, t_w, t_b), (wait_src, ws_w, ws_b), (wait_dst, wd_w, wd_b))):
-            nc.scalar.dma_start(out=num_wb[32 * t : 32 * t + 1, t, :], in_=row(w_t))
-            nc.scalar.dma_start(out=num_wb[96:97, t, :], in_=row(b_t))
-            nc.scalar.dma_start(out=rows_num[32 * t : 32 * t + 1, :], in_=row(scal))
+        num_wb = keep.tile([P, 3, P], BF16)
+        nc.vector.memset(num_wb[:], 0.0)
+        nc.gpsimd.dma_start(out=rows_num[64:65, :], in_=row(wait_dst))
+        load(rows_num[0:1, :], row(time_s))
+        load(rows_num[32:33, :], row(wait_src))
+        for t, (w_t, b_t) in enumerate(((t_w, t_b), (ws_w, ws_b), (wd_w, wd_b))):
+            load(num_wb[32 * t : 32 * t + 1, t, :], row(w_t))
+            load(num_wb[96:97, t, :], row(b_t))
+        w1n = keep.tile([P, 3, H], BF16)
+        nc.gpsimd.dma_start(out=w1n[:], in_=W1[640:1024, :].rearrange("(t p) n -> p t n", p=P))
+        w2 = keep.tile([P, 4, H], BF16)
+        nc.gpsimd.dma_start(out=w2[:], in_=W2.rearrange("(t p) n -> p t n", p=P))
+
+        g_c = keep.tile([P, CH, 4], BF16, align_bytes=64)
+        nc.vector.memset(g_c[:], 0.0)
+        rows_xy = keep.tile([P, 2 * B], BF16)
+        nc.vector.memset(rows_xy[:], 0.0)
+        flat_s = src_xy.rearrange("b c -> (b c)")
+        flat_d = dst_xy.rearrange("b c -> (b c)")
+        load(rows_xy[0:1, :], row(flat_s))
+        load(rows_xy[32:33, 0 : 2 * B - 1], row(flat_s[1 : 2 * B]))
+        load(rows_xy[64:65, :], row(flat_d))
+        load(rows_xy[96:97, 0 : 2 * B - 1], row(flat_d[1 : 2 * B]))
 
         pw = keep.tile([P, SLOTS], BF16)
         pb = keep.tile([P, SLOTS], BF16)
@@ -77,115 +98,77 @@ def tile_claimencoder_kernel(
         )
         for g, (w_sin, b_sin, w_cos, b_cos) in enumerate(groups):
             lo = 32 * g
-            nc.sync.dma_start(out=pw[lo : lo + 16, :], in_=w_sin.rearrange("(l s) -> l s", s=SLOTS))
-            nc.sync.dma_start(out=pw[lo + 16 : lo + 32, :], in_=w_cos.rearrange("(l s) -> l s", s=SLOTS))
-            nc.gpsimd.dma_start(out=pb[lo : lo + 16, :], in_=b_sin.rearrange("(l s) -> l s", s=SLOTS))
-            nc.gpsimd.dma_start(out=pb[lo + 16 : lo + 32, :], in_=b_cos.rearrange("(l s) -> l s", s=SLOTS))
-
-        rows_xy = keep.tile([P, 2 * B], BF16)
-        nc.vector.memset(rows_xy[:], 0.0)
-        flat_s = src_xy.rearrange("b c -> (b c)")
-        flat_d = dst_xy.rearrange("b c -> (b c)")
-        nc.scalar.dma_start(out=rows_xy[0:1, :], in_=row(flat_s))
-        nc.scalar.dma_start(out=rows_xy[32:33, 0 : 2 * B - 1], in_=row(flat_s[1 : 2 * B]))
-        nc.scalar.dma_start(out=rows_xy[64:65, :], in_=row(flat_d))
-        nc.scalar.dma_start(out=rows_xy[96:97, 0 : 2 * B - 1], in_=row(flat_d[1 : 2 * B]))
-
-        w2 = keep.tile([P, 4, H], BF16)
-        nc.sync.dma_start(out=w2[:], in_=W2.rearrange("(t p) n -> p t n", p=P))
+            load(pw[lo : lo + 16, :], w_sin.rearrange("(l s) -> l s", s=SLOTS))
+            load(pw[lo + 16 : lo + 32, :], w_cos.rearrange("(l s) -> l s", s=SLOTS))
+            load(pb[lo : lo + 16, :], b_sin.rearrange("(l s) -> l s", s=SLOTS))
+            load(pb[lo + 16 : lo + 32, :], b_cos.rearrange("(l s) -> l s", s=SLOTS))
         b1raw = keep.tile([P, 4], BF16)
         with nc.allow_non_contiguous_dma(reason="512 bias values, one per partition and output tile"):
-            nc.sync.dma_start(out=b1raw[:], in_=b1.rearrange("(m p) -> p m", p=P))
+            load(b1raw[:], b1.rearrange("(m p) -> p m", p=P))
         b2bc = keep.tile([P, H], BF16)
-        nc.sync.dma_start(out=b2bc[:], in_=b2.partition_broadcast(P))
+        load(b2bc[:], b2.partition_broadcast(P))
 
         sel = keep.tile([P, P], BF16)
         nc.vector.memset(sel[:], 0.0)
         for g in range(4):
             nc.vector.memset(sel[32 * g : 32 * g + 32, 32 * g : 32 * g + 32], 1.0)
-
-        g_b = keep.tile([P, CH, 4], BF16, align_bytes=64)
-        g_c = keep.tile([P, CH, 4], BF16, align_bytes=64)
-        nc.gpsimd.memset(g_c[:].rearrange("p n t -> p (n t)").bitcast(F32), 0.0)
-        nc.gpsimd.memset(g_b[:].rearrange("p n t -> p (n t)").bitcast(F32), 0.0)
+        g_wc = keep.tile([P, H, 4], BF16, align_bytes=64)
+        nc.vector.memset(g_wc[:], 0.0)
 
         lane = keep.tile([P, 1], I32)
         nc.gpsimd.iota(lane[:], pattern=[[0, 1]], base=0, channel_multiplier=1)
-        bit = keep.tile([P, 1], I32)
-        nc.vector.tensor_scalar(out=bit[:], in0=lane[:], scalar1=16, scalar2=None, op0=ALU.bitwise_and)
-        phase = keep.tile([P, 1], F32)
-        nc.vector.tensor_scalar(out=phase[:], in0=bit[:], scalar1=math.pi / 32.0, scalar2=None, op0=ALU.mult)
-        wq = keep.tile([P, SLOTS], F32)
-        nc.vector.tensor_scalar(out=wq[:], in0=pw[:], scalar1=1.0 / TWO_PI, scalar2=None, op0=ALU.mult)
-        sb = keep.tile([P, SLOTS], F32)
-        nc.vector.tensor_scalar(out=sb[:], in0=pb[:], scalar1=phase[:, 0:1], scalar2=None, op0=ALU.add)
-        bq = keep.tile([P, SLOTS], F32)
-        nc.vector.tensor_scalar(out=bq[:], in0=sb[:], scalar1=1.0 / TWO_PI, scalar2=None, op0=ALU.mult)
-        b1f = keep.tile([P, 4], F32)
-        nc.vector.tensor_copy(out=b1f[:], in_=b1raw[:])
-        b1s = keep.tile([P, 4], F32)
-        nc.vector.tensor_scalar(out=b1s[:], in0=b1raw[:], scalar1=SLOPE, scalar2=None, op0=ALU.mult)
+        g_wb = keep.tile([P, H, 4], BF16, align_bytes=64)
+        nc.gpsimd.memset(g_wb[:].rearrange("p n t -> p (n t)").bitcast(F32), 0.0)
+        g_bs = []
+        for c in range(NCH):
+            g_b = keep.tile([P, CH, 4], BF16, name="g_b%d" % c, align_bytes=64)
+            nc.gpsimd.memset(g_b[:].rearrange("p n t -> p (n t)").bitcast(F32), 0.0)
+            g_bs.append(g_b)
 
         cw = keep.tile([P, 4, H], U32, align_bytes=64)
         sw = keep.tile([P, 4, H], U8, align_bytes=64)
+        cf = keep.tile([P, 3, B], U32, align_bytes=64)
+        sf = keep.tile([P, 3, B], U8, align_bytes=64)
+        xs = keep.tile([P, B], BF16)
+        wq = keep.tile([P, SLOTS], F32)
+        sb = keep.tile([P, SLOTS], F32)
+        bq = keep.tile([P, SLOTS], F32)
+        b1f = keep.tile([P, 4], F32)
 
         def quantise(codes, scales, grouped):
             nc.vector.quantize_mx(
                 out=codes.bitcast(FP8X4), scales=scales, in_=grouped.rearrange("p n t -> p (n t)")
             )
 
-        g_w1 = work.tile([P, H, 4], BF16, tag="g_a", align_bytes=64)
-        regroup(nc.vector.tensor_copy, g_w1[:], w1s[:, 0:4, :])
-        nc.scalar.copy(out=g_b[:, :, 0], in_=w1s[:, 4, :])
-        regroup(nc.scalar.copy, g_c[:, :, 0:3], w1n[:])
-        g_w2 = work.tile([P, H, 4], BF16, tag="g_a", align_bytes=64)
-        regroup(nc.scalar.copy, g_w2[:], w2[:])
-        quantise(cw[:, 0, :], sw[:, 0, :], g_w1[:])
-        quantise(cw[:, 1, :], sw[:, 1, :], g_b[:])
-        quantise(cw[:, 2, :], sw[:, 2, :], g_c[:])
-        quantise(cw[:, 3, :], sw[:, 3, :], g_w2[:])
+        def constants():
+            bit = keep.tile([P, 1], I32)
+            nc.vector.tensor_scalar(out=bit[:], in0=lane[:], scalar1=16, scalar2=None, op0=ALU.bitwise_and)
+            phase = keep.tile([P, 1], F32)
+            nc.vector.tensor_scalar(out=phase[:], in0=bit[:], scalar1=math.pi / 32.0, scalar2=None, op0=ALU.mult)
+            nc.vector.tensor_scalar(out=wq[:], in0=pw[:], scalar1=1.0 / TWO_PI, scalar2=None, op0=ALU.mult)
+            nc.vector.tensor_scalar(out=sb[:], in0=pb[:], scalar1=phase[:, 0:1], scalar2=None, op0=ALU.add)
+            nc.vector.tensor_scalar(out=bq[:], in0=sb[:], scalar1=1.0 / TWO_PI, scalar2=None, op0=ALU.mult)
+            nc.vector.tensor_copy(out=b1f[:], in_=b1raw[:])
 
-        xs = keep.tile([P, B], BF16)
-        pairs = rows_xy[:].rearrange("p (b c) -> p b c", c=2)
-        for c in range(NCH):
-            xps = ps3.tile([P, CH], F32, tag="ps3")
-            nc.tensor.matmul(out=xps[:], lhsT=sel[:], rhs=pairs[:, c * CH : (c + 1) * CH, 0], start=True, stop=True)
-            nc.scalar.copy(out=xs[:, c * CH : (c + 1) * CH], in_=xps[:])
-
-        cf = keep.tile([P, 3, B], U32, align_bytes=64)
-        sf = keep.tile([P, 3, B], U8, align_bytes=64)
-
-        def features(c):
-            cs = slice(c * CH, (c + 1) * CH)
-            planes = work.tile([P, 4, CH], BF16, tag="planes")
-            for s in range(SLOTS):
-                turns = work.tile([P, CH], I32, tag="turns", bufs=3)
-                nc.vector.tensor_scalar(
-                    out=turns[:], in0=xs[:, cs], scalar1=wq[:, s : s + 1], scalar2=bq[:, s : s + 1],
-                    op0=ALU.mult, op1=ALU.add,
+        def spread_points():
+            pairs = rows_xy[:].rearrange("p (b c) -> p b c", c=2)
+            for c in range(NCH):
+                xps = psum.tile([P, CH], F32, tag="bank")
+                nc.tensor.matmul(
+                    out=xps[:], lhsT=sel[:], rhs=pairs[:, c * CH : (c + 1) * CH, 0], start=True, stop=True
                 )
-                frac = work.tile([P, CH], F32, tag="frac", bufs=4)
-                nc.vector.scalar_tensor_tensor(
-                    out=frac[:], in0=xs[:, cs], scalar=wq[:, s : s + 1], in1=turns[:],
-                    op0=ALU.mult, op1=ALU.subtract,
-                )
-                dst = planes[:, s, :] if s < 4 else g_b[:, :, 0]
-                nc.scalar.activation(out=dst, in_=frac[:], func=ACT.Sin, bias=sb[:, s : s + 1], scale=TWO_PI)
-            g_a = work.tile([P, CH, 4], BF16, tag="g_a", align_bytes=64)
-            regroup(nc.scalar.copy, g_a[:], planes[:])
-            quantise(cf[:, 0, cs], sf[:, 0, cs], g_a[:])
-            quantise(cf[:, 1, cs], sf[:, 1, cs], g_b[:])
+                nc.scalar.copy(out=xs[:, c * CH : (c + 1) * CH], in_=xps[:])
 
         def num_features(c):
             cs = slice(c * CH, (c + 1) * CH)
             for j in range(CH // P):
-                vps = ps3.tile([P, 4, P], F32, tag="ps3")
+                vps = psum.tile([P, 4, P], F32, tag="bank")
                 lo = c * CH + j * P
                 for t in range(3):
                     nc.tensor.matmul(
                         out=vps[:, t, :], lhsT=num_wb[:, t, :], rhs=rows_num[:, lo : lo + P], start=True, stop=True
                     )
-                small = work.tile([P, 3, P], F32, tag="small", bufs=3)
+                small = work.tile([P, 3, P], F32, tag="small", bufs=4)
                 nc.scalar.activation(out=small[:], in_=vps[:, 0:3, :], func=ACT.Copy, scale=SLOPE)
                 nc.vector.tensor_tensor(
                     out=g_c[:, j * P : (j + 1) * P, 0:3],
@@ -195,16 +178,41 @@ def tile_claimencoder_kernel(
                 )
             quantise(cf[:, 2, cs], sf[:, 2, cs], g_c[:])
 
-        hidden = {}
+        grouped_a = {}
+
+        def sin_features(c):
+            cs = slice(c * CH, (c + 1) * CH)
+            planes = work.tile([P, 4, CH], BF16, tag="planes")
+            for s in range(SLOTS):
+                turns = work.tile([P, CH], I32, tag="turns", bufs=3)
+                nc.vector.tensor_scalar(
+                    out=turns[:], in0=xs[:, cs], scalar1=wq[:, s : s + 1], scalar2=bq[:, s : s + 1],
+                    op0=ALU.mult, op1=ALU.add,
+                )
+                frac = work.tile([P, CH], F32, tag="frac", bufs=6)
+                nc.vector.scalar_tensor_tensor(
+                    out=frac[:], in0=xs[:, cs], scalar=wq[:, s : s + 1], in1=turns[:],
+                    op0=ALU.mult, op1=ALU.subtract,
+                )
+                dst = planes[:, s, :] if s < 4 else g_bs[c][:, :, 0]
+                nc.scalar.activation(out=dst, in_=frac[:], func=ACT.Sin, bias=sb[:, s : s + 1], scale=TWO_PI)
+            g_a = work.tile([P, CH, 4], BF16, tag="g_a", bufs=3, align_bytes=64)
+            regroup(nc.scalar.copy, g_a[:], planes[:])
+            grouped_a[c] = g_a
+
+        def quantise_sin(c):
+            cs = slice(c * CH, (c + 1) * CH)
+            quantise(cf[:, 0, cs], sf[:, 0, cs], grouped_a[c][:])
+            quantise(cf[:, 1, cs], sf[:, 1, cs], g_bs[c][:])
+
+        biased = {}
 
         def layer1(c):
             cs = slice(c * CH, (c + 1) * CH)
-            hp = work.tile([P, 4, CH], BF16, tag="hp")
-            up = work.tile([P, 4, CH], BF16, tag="up")
-            low = work.tile([P, 4, CH], BF16, tag="low")
+            pre1 = work.tile([P, 4, CH], F32, tag="pre1")
             for m in range(4):
                 ms = slice(m * P, (m + 1) * P)
-                acc = ps1.tile([P, CH], F32, tag="acc1")
+                acc = psum.tile([P, CH], F32, tag="bank")
                 for i in range(3):
                     nc.tensor.matmul_mx(
                         out=acc[:],
@@ -212,11 +220,17 @@ def tile_claimencoder_kernel(
                         rhs=cf[:, i, cs].bitcast(FP8X4), rhs_scale=sf[:, i, cs],
                         start=(i == 0), stop=(i == 2),
                     )
-                nc.scalar.activation(out=up[:, m, :], in_=acc[:], func=ACT.Identity, bias=b1f[:, m : m + 1], scale=1.0)
-                nc.scalar.activation(out=low[:, m, :], in_=acc[:], func=ACT.Identity, bias=b1s[:, m : m + 1], scale=SLOPE)
-            nc.vector.tensor_tensor(out=hp[:], in0=up[:], in1=low[:], op=ALU.max)
+                nc.scalar.activation(out=pre1[:, m, :], in_=acc[:], func=ACT.Identity, bias=b1f[:, m : m + 1], scale=1.0)
+            biased[c] = pre1
+
+        hidden = {}
+
+        def hidden_codes(c):
+            by_claim = biased[c][:].rearrange("p t b -> p b t")
             g_h = work.tile([P, CH, 4], BF16, tag="g_h", align_bytes=64)
-            regroup(nc.scalar.copy, g_h[:], hp[:])
+            nc.vector.scalar_tensor_tensor(
+                out=g_h[:], in0=by_claim, scalar=SLOPE, in1=by_claim, op0=ALU.mult, op1=ALU.max
+            )
             ch = work.tile([P, CH], U32, tag="ch", align_bytes=64)
             sh = work.tile([P, CH], U8, tag="sh", align_bytes=64)
             quantise(ch[:], sh[:], g_h[:])
@@ -226,7 +240,7 @@ def tile_claimencoder_kernel(
             ch, sh = hidden[c]
             for j in range(CH // P):
                 js = slice(j * P, (j + 1) * P)
-                acc = ps2.tile([P, H], F32, tag="acc2")
+                acc = psum.tile([P, H], F32, tag="bank")
                 nc.tensor.matmul_mx(
                     out=acc[:],
                     lhsT=ch[:, js].bitcast(FP8X4), lhsT_scale=sh[:, js],
@@ -235,7 +249,7 @@ def tile_claimencoder_kernel(
                 )
                 pre = work.tile([P, H], F32, tag="pre", bufs=3)
                 nc.vector.tensor_tensor(out=pre[:], in0=acc[:], in1=b2bc[:], op=ALU.add)
-                res = work.tile([P, H], F32, tag="res", bufs=3)
+                res = work.tile([P, H], F32, tag="res", bufs=4)
                 nc.vector.scalar_tensor_tensor(
                     out=res[:], in0=pre[:], scalar=SLOPE, in1=pre[:], op0=ALU.mult, op1=ALU.max
                 )
@@ -243,14 +257,32 @@ def tile_claimencoder_kernel(
                 nc.sync.dma_start(out=out[lo : lo + P, :], in_=res[:])
 
         num_features(0)
-        features(0)
+        g_w1 = work.tile([P, H, 4], BF16, tag="g_a", bufs=3, align_bytes=64)
+        regroup(nc.vector.tensor_copy, g_w1[:], w1s[:, 0:4, :])
+        regroup(nc.scalar.copy, g_wc[:, :, 0:3], w1n[:])
+        nc.scalar.copy(out=g_wb[:, :, 0], in_=w1s[:, 4, :])
+        quantise(cw[:, 0, :], sw[:, 0, :], g_w1[:])
+        quantise(cw[:, 2, :], sw[:, 2, :], g_wc[:])
+        quantise(cw[:, 1, :], sw[:, 1, :], g_wb[:])
         num_features(1)
-        features(1)
-        layer1(0)
         num_features(2)
-        features(2)
-        layer2(0)
+        spread_points()
+        g_w2 = keep.tile([P, H, 4], BF16, align_bytes=64)
+        regroup(nc.scalar.copy, g_w2[:], w2[:])
+        constants()
+        sin_features(0)
+        sin_features(1)
+        quantise_sin(0)
+        layer1(0)
+        sin_features(2)
+        quantise(cw[:, 3, :], sw[:, 3, :], g_w2[:])
+        quantise_sin(1)
         layer1(1)
-        layer2(1)
+        hidden_codes(0)
+        layer2(0)
+        quantise_sin(2)
         layer1(2)
+        hidden_codes(1)
+        layer2(1)
+        hidden_codes(2)
         layer2(2)

@@ -61,17 +61,17 @@ def tile_claimencoder_kernel(
         nc.vector.memset(warm[:], 0.0)
         warmed = keep.tile([P, 1], F32)
         nc.scalar.activation(out=warmed[:], in_=warm[:], func=ACT.Sin)
-        rows_num = keep.tile([P, B], BF16)
-        nc.vector.memset(rows_num[:], 0.0)
-        nc.vector.memset(rows_num[96:128, :], 1.0)
         num_wb = keep.tile([P, 3, P], BF16)
         nc.vector.memset(num_wb[:], 0.0)
-        nc.gpsimd.dma_start(out=rows_num[64:65, :], in_=row(wait_dst))
-        load(rows_num[0:1, :], row(time_s))
-        load(rows_num[32:33, :], row(wait_src))
         for t, (w_t, b_t) in enumerate(((t_w, t_b), (ws_w, ws_b), (wd_w, wd_b))):
             load(num_wb[32 * t : 32 * t + 1, t, :], row(w_t))
             load(num_wb[96:97, t, :], row(b_t))
+        rows_num = keep.tile([P, B], BF16)
+        nc.vector.memset(rows_num[:], 0.0)
+        nc.vector.memset(rows_num[96:128, :], 1.0)
+        nc.gpsimd.dma_start(out=rows_num[64:65, :], in_=row(wait_dst))
+        load(rows_num[0:1, :], row(time_s))
+        load(rows_num[32:33, :], row(wait_src))
         w1n = keep.tile([P, 3, H], BF16)
         nc.gpsimd.dma_start(out=w1n[:], in_=W1[640:1024, :].rearrange("(t p) n -> p t n", p=P))
         w2 = keep.tile([P, 4, H], BF16)
@@ -159,8 +159,10 @@ def tile_claimencoder_kernel(
                 )
                 nc.scalar.copy(out=xs[:, c * CH : (c + 1) * CH], in_=xps[:])
 
-        def num_features(c):
-            cs = slice(c * CH, (c + 1) * CH)
+        banks = {}
+        smalls = {}
+
+        def num_products(c):
             for j in range(CH // P):
                 vps = psum.tile([P, 4, P], F32, tag="bank")
                 lo = c * CH + j * P
@@ -168,47 +170,73 @@ def tile_claimencoder_kernel(
                     nc.tensor.matmul(
                         out=vps[:, t, :], lhsT=num_wb[:, t, :], rhs=rows_num[:, lo : lo + P], start=True, stop=True
                     )
-                small = work.tile([P, 3, P], F32, tag="small", bufs=4)
+                small = work.tile([P, 3, P], F32, tag="small", bufs=8)
                 nc.scalar.activation(out=small[:], in_=vps[:, 0:3, :], func=ACT.Copy, scale=SLOPE)
+                banks[(c, j)] = vps
+                smalls[(c, j)] = small
+
+        def num_leaky(c):
+            for j in range(CH // P):
                 nc.vector.tensor_tensor(
                     out=g_c[:, j * P : (j + 1) * P, 0:3],
-                    in0=vps[:, 0:3, :].rearrange("p t b -> p b t"),
-                    in1=small[:].rearrange("p t b -> p b t"),
+                    in0=banks[(c, j)][:, 0:3, :].rearrange("p t b -> p b t"),
+                    in1=smalls[(c, j)][:].rearrange("p t b -> p b t"),
                     op=ALU.max,
                 )
-            quantise(cf[:, 2, cs], sf[:, 2, cs], g_c[:])
 
+        def chunk(c):
+            return slice(c * CH, (c + 1) * CH)
+
+        def quantise_num(c):
+            quantise(cf[:, 2, chunk(c)], sf[:, 2, chunk(c)], g_c[:])
+
+        turn_tiles = {}
+        plane_tiles = {}
         grouped_a = {}
 
-        def sin_features(c):
-            cs = slice(c * CH, (c + 1) * CH)
-            planes = work.tile([P, 4, CH], BF16, tag="planes")
-            for s in range(SLOTS):
-                turns = work.tile([P, CH], I32, tag="turns", bufs=3)
-                nc.vector.tensor_scalar(
-                    out=turns[:], in0=xs[:, cs], scalar1=wq[:, s : s + 1], scalar2=bq[:, s : s + 1],
-                    op0=ALU.mult, op1=ALU.add,
-                )
-                frac = work.tile([P, CH], F32, tag="frac", bufs=6)
-                nc.vector.scalar_tensor_tensor(
-                    out=frac[:], in0=xs[:, cs], scalar=wq[:, s : s + 1], in1=turns[:],
-                    op0=ALU.mult, op1=ALU.subtract,
-                )
-                dst = planes[:, s, :] if s < 4 else g_bs[c][:, :, 0]
-                nc.scalar.activation(out=dst, in_=frac[:], func=ACT.Sin, bias=sb[:, s : s + 1], scale=TWO_PI)
-            g_a = work.tile([P, CH, 4], BF16, tag="g_a", bufs=3, align_bytes=64)
-            regroup(nc.scalar.copy, g_a[:], planes[:])
-            grouped_a[c] = g_a
+        def count_turns(c, s):
+            turns = work.tile([P, CH], I32, tag="turns", bufs=4)
+            nc.vector.tensor_scalar(
+                out=turns[:], in0=xs[:, chunk(c)], scalar1=wq[:, s : s + 1], scalar2=bq[:, s : s + 1],
+                op0=ALU.mult, op1=ALU.add,
+            )
+            turn_tiles[(c, s)] = turns
+
+        def sine(c, s):
+            frac = work.tile([P, CH], F32, tag="frac", bufs=6)
+            nc.vector.scalar_tensor_tensor(
+                out=frac[:], in0=xs[:, chunk(c)], scalar=wq[:, s : s + 1], in1=turn_tiles[(c, s)][:],
+                op0=ALU.mult, op1=ALU.subtract,
+            )
+            if s == 0:
+                planes = work.tile([P, 4, CH], BF16, tag="planes")
+                plane_tiles[c] = planes
+            dst = plane_tiles[c][:, s, :] if s < 4 else g_bs[c][:, :, 0]
+            nc.scalar.activation(out=dst, in_=frac[:], func=ACT.Sin, bias=sb[:, s : s + 1], scale=TWO_PI)
+            if s == 4:
+                g_a = work.tile([P, CH, 4], BF16, tag="g_a", bufs=3, align_bytes=64)
+                regroup(nc.scalar.copy, g_a[:], plane_tiles[c][:])
+                grouped_a[c] = g_a
+
+        slots = [(c, s) for c in range(NCH) for s in range(SLOTS)]
+        done = []
+
+        def sine_stream(steps):
+            for step in range(steps):
+                i = len(done)
+                if i < len(slots):
+                    count_turns(slots[i][0], slots[i][1])
+                if 0 < i <= len(slots):
+                    sine(slots[i - 1][0], slots[i - 1][1])
+                done.append(i)
 
         def quantise_sin(c):
-            cs = slice(c * CH, (c + 1) * CH)
-            quantise(cf[:, 0, cs], sf[:, 0, cs], grouped_a[c][:])
-            quantise(cf[:, 1, cs], sf[:, 1, cs], g_bs[c][:])
+            quantise(cf[:, 0, chunk(c)], sf[:, 0, chunk(c)], grouped_a[c][:])
+            quantise(cf[:, 1, chunk(c)], sf[:, 1, chunk(c)], g_bs[c][:])
 
         biased = {}
 
         def layer1(c):
-            cs = slice(c * CH, (c + 1) * CH)
             pre1 = work.tile([P, 4, CH], F32, tag="pre1")
             for m in range(4):
                 ms = slice(m * P, (m + 1) * P)
@@ -217,24 +245,31 @@ def tile_claimencoder_kernel(
                     nc.tensor.matmul_mx(
                         out=acc[:],
                         lhsT=cw[:, i, ms].bitcast(FP8X4), lhsT_scale=sw[:, i, ms],
-                        rhs=cf[:, i, cs].bitcast(FP8X4), rhs_scale=sf[:, i, cs],
+                        rhs=cf[:, i, chunk(c)].bitcast(FP8X4), rhs_scale=sf[:, i, chunk(c)],
                         start=(i == 0), stop=(i == 2),
                     )
                 nc.scalar.activation(out=pre1[:, m, :], in_=acc[:], func=ACT.Identity, bias=b1f[:, m : m + 1], scale=1.0)
             biased[c] = pre1
 
+        grouped_h = {}
         hidden = {}
 
-        def hidden_codes(c):
+        def hidden_leaky(c):
             by_claim = biased[c][:].rearrange("p t b -> p b t")
             g_h = work.tile([P, CH, 4], BF16, tag="g_h", align_bytes=64)
             nc.vector.scalar_tensor_tensor(
                 out=g_h[:], in0=by_claim, scalar=SLOPE, in1=by_claim, op0=ALU.mult, op1=ALU.max
             )
+            grouped_h[c] = g_h
+
+        def quantise_hidden(c):
             ch = work.tile([P, CH], U32, tag="ch", align_bytes=64)
             sh = work.tile([P, CH], U8, tag="sh", align_bytes=64)
-            quantise(ch[:], sh[:], g_h[:])
+            quantise(ch[:], sh[:], grouped_h[c][:])
             hidden[c] = (ch, sh)
+
+        sums = {}
+        pres = {}
 
         def layer2(c):
             ch, sh = hidden[c]
@@ -247,42 +282,67 @@ def tile_claimencoder_kernel(
                     rhs=cw[:, 3, :].bitcast(FP8X4), rhs_scale=sw[:, 3, :],
                     start=True, stop=True,
                 )
-                pre = work.tile([P, H], F32, tag="pre", bufs=3)
-                nc.vector.tensor_tensor(out=pre[:], in0=acc[:], in1=b2bc[:], op=ALU.add)
-                res = work.tile([P, H], F32, tag="res", bufs=4)
-                nc.vector.scalar_tensor_tensor(
-                    out=res[:], in0=pre[:], scalar=SLOPE, in1=pre[:], op0=ALU.mult, op1=ALU.max
-                )
-                lo = c * CH + j * P
-                nc.sync.dma_start(out=out[lo : lo + P, :], in_=res[:])
+                sums[(c, j)] = acc
 
-        num_features(0)
-        g_w1 = work.tile([P, H, 4], BF16, tag="g_a", bufs=3, align_bytes=64)
-        regroup(nc.vector.tensor_copy, g_w1[:], w1s[:, 0:4, :])
+        def add_bias(c, j):
+            pre = work.tile([P, H], F32, tag="pre", bufs=4)
+            nc.vector.tensor_tensor(out=pre[:], in0=sums[(c, j)][:], in1=b2bc[:], op=ALU.add)
+            pres[(c, j)] = pre
+
+        def finish(c, j):
+            res = work.tile([P, H], F32, tag="res", bufs=4)
+            pre = pres[(c, j)]
+            nc.vector.scalar_tensor_tensor(
+                out=res[:], in0=pre[:], scalar=SLOPE, in1=pre[:], op0=ALU.mult, op1=ALU.max
+            )
+            lo = c * CH + j * P
+            nc.sync.dma_start(out=out[lo : lo + P, :], in_=res[:])
+
+        def outputs(c, between):
+            layer2(c)
+            add_bias(c, 0)
+            add_bias(c, 1)
+            finish(c, 0)
+            add_bias(c, 2)
+            finish(c, 1)
+            add_bias(c, 3)
+            finish(c, 2)
+            for step in between:
+                step[0](step[1])
+            finish(c, 3)
+
+        num_products(0)
+        num_leaky(0)
         regroup(nc.scalar.copy, g_wc[:, :, 0:3], w1n[:])
         nc.scalar.copy(out=g_wb[:, :, 0], in_=w1s[:, 4, :])
+        g_w1 = keep.tile([P, H, 4], BF16, align_bytes=64)
+        regroup(nc.vector.tensor_copy, g_w1[:], w1s[:, 0:4, :])
+        quantise_num(0)
+        num_products(1)
         quantise(cw[:, 0, :], sw[:, 0, :], g_w1[:])
+        num_leaky(1)
         quantise(cw[:, 2, :], sw[:, 2, :], g_wc[:])
+        quantise_num(1)
+        num_products(2)
         quantise(cw[:, 1, :], sw[:, 1, :], g_wb[:])
-        num_features(1)
-        num_features(2)
+        num_leaky(2)
         spread_points()
         g_w2 = keep.tile([P, H, 4], BF16, align_bytes=64)
         regroup(nc.scalar.copy, g_w2[:], w2[:])
         constants()
-        sin_features(0)
-        sin_features(1)
+        quantise_num(2)
+        sine_stream(11)
         quantise_sin(0)
         layer1(0)
-        sin_features(2)
+        sine_stream(5)
         quantise(cw[:, 3, :], sw[:, 3, :], g_w2[:])
         quantise_sin(1)
         layer1(1)
-        hidden_codes(0)
-        layer2(0)
-        quantise_sin(2)
-        layer1(2)
-        hidden_codes(1)
-        layer2(1)
-        hidden_codes(2)
-        layer2(2)
+        hidden_leaky(0)
+        quantise_hidden(0)
+        outputs(0, ((quantise_sin, 2), (layer1, 2)))
+        hidden_leaky(1)
+        quantise_hidden(1)
+        outputs(1, ((hidden_leaky, 2),))
+        quantise_hidden(2)
+        outputs(2, ())

@@ -148,7 +148,6 @@ def tile_claimencoder_kernel(
             nc.vector.tensor_scalar(out=wq[:], in0=pw[:], scalar1=1.0 / TWO_PI, scalar2=None, op0=ALU.mult)
             nc.vector.tensor_scalar(out=sb[:], in0=pb[:], scalar1=phase[:, 0:1], scalar2=None, op0=ALU.add)
             nc.vector.tensor_scalar(out=bq[:], in0=sb[:], scalar1=1.0 / TWO_PI, scalar2=None, op0=ALU.mult)
-            nc.vector.tensor_copy(out=b1f[:], in_=b1raw[:])
 
         def spread_points():
             pairs = rows_xy[:].rearrange("p (b c) -> p b c", c=2)
@@ -254,35 +253,42 @@ def tile_claimencoder_kernel(
         grouped_h = {}
         hidden = {}
 
-        def hidden_leaky(c):
-            by_claim = biased[c][:].rearrange("p t b -> p b t")
-            g_h = work.tile([P, CH, 4], BF16, tag="g_h", align_bytes=64)
-            nc.vector.scalar_tensor_tensor(
-                out=g_h[:], in0=by_claim, scalar=SLOPE, in1=by_claim, op0=ALU.mult, op1=ALU.max
-            )
-            grouped_h[c] = g_h
+        HALF = CH // 2
 
-        def quantise_hidden(c):
-            ch = work.tile([P, CH], U32, tag="ch", align_bytes=64)
-            sh = work.tile([P, CH], U8, tag="sh", align_bytes=64)
-            quantise(ch[:], sh[:], grouped_h[c][:])
-            hidden[c] = (ch, sh)
+        def hidden_leaky(c, half):
+            if half == 0:
+                g_h = work.tile([P, CH, 4], BF16, tag="g_h", align_bytes=64)
+                grouped_h[c] = g_h
+            hs = slice(half * HALF, (half + 1) * HALF)
+            by_claim = biased[c][:].rearrange("p t b -> p b t")[:, hs, :]
+            nc.vector.scalar_tensor_tensor(
+                out=grouped_h[c][:, hs, :], in0=by_claim, scalar=SLOPE, in1=by_claim, op0=ALU.mult, op1=ALU.max
+            )
+
+        def quantise_hidden(c, half):
+            if half == 0:
+                ch = work.tile([P, CH], U32, tag="ch", align_bytes=64)
+                sh = work.tile([P, CH], U8, tag="sh", align_bytes=64)
+                hidden[c] = (ch, sh)
+            hs = slice(half * HALF, (half + 1) * HALF)
+            quantise(hidden[c][0][:, hs], hidden[c][1][:, hs], grouped_h[c][:, hs, :])
+            layer2(c, 2 * half)
+            layer2(c, 2 * half + 1)
 
         sums = {}
         pres = {}
 
-        def layer2(c):
+        def layer2(c, j):
             ch, sh = hidden[c]
-            for j in range(CH // P):
-                js = slice(j * P, (j + 1) * P)
-                acc = psum.tile([P, H], F32, tag="bank")
-                nc.tensor.matmul_mx(
-                    out=acc[:],
-                    lhsT=ch[:, js].bitcast(FP8X4), lhsT_scale=sh[:, js],
-                    rhs=cw[:, 3, :].bitcast(FP8X4), rhs_scale=sw[:, 3, :],
-                    start=True, stop=True,
-                )
-                sums[(c, j)] = acc
+            js = slice(j * P, (j + 1) * P)
+            acc = psum.tile([P, H], F32, tag="bank")
+            nc.tensor.matmul_mx(
+                out=acc[:],
+                lhsT=ch[:, js].bitcast(FP8X4), lhsT_scale=sh[:, js],
+                rhs=cw[:, 3, :].bitcast(FP8X4), rhs_scale=sw[:, 3, :],
+                start=True, stop=True,
+            )
+            sums[(c, j)] = acc
 
         def add_bias(c, j):
             pre = work.tile([P, H], F32, tag="pre", bufs=4)
@@ -298,51 +304,58 @@ def tile_claimencoder_kernel(
             lo = c * CH + j * P
             nc.sync.dma_start(out=out[lo : lo + P, :], in_=res[:])
 
-        def outputs(c, between):
-            layer2(c)
+        def outputs(c, before_third, before_last):
             add_bias(c, 0)
             add_bias(c, 1)
             finish(c, 0)
             add_bias(c, 2)
             finish(c, 1)
             add_bias(c, 3)
+            for step in before_third:
+                step()
             finish(c, 2)
-            for step in between:
-                step[0](step[1])
+            for step in before_last:
+                step()
             finish(c, 3)
 
+        def hidden_all(c):
+            hidden_leaky(c, 0)
+            hidden_leaky(c, 1)
+            quantise_hidden(c, 0)
+            quantise_hidden(c, 1)
+
         num_products(0)
-        num_leaky(0)
-        regroup(nc.scalar.copy, g_wc[:, :, 0:3], w1n[:])
-        nc.scalar.copy(out=g_wb[:, :, 0], in_=w1s[:, 4, :])
+        num_products(1)
         g_w1 = keep.tile([P, H, 4], BF16, align_bytes=64)
         regroup(nc.vector.tensor_copy, g_w1[:], w1s[:, 0:4, :])
-        quantise_num(0)
-        num_products(1)
+        num_leaky(0)
         quantise(cw[:, 0, :], sw[:, 0, :], g_w1[:])
+        quantise_num(0)
         num_leaky(1)
+        regroup(nc.scalar.copy, g_wc[:, :, 0:3], w1n[:])
+        num_products(2)
+        nc.scalar.copy(out=g_wb[:, :, 0], in_=w1s[:, 4, :])
+        spread_points()
         quantise(cw[:, 2, :], sw[:, 2, :], g_wc[:])
         quantise_num(1)
-        num_products(2)
-        quantise(cw[:, 1, :], sw[:, 1, :], g_wb[:])
         num_leaky(2)
-        spread_points()
+        quantise(cw[:, 1, :], sw[:, 1, :], g_wb[:])
         g_w2 = keep.tile([P, H, 4], BF16, align_bytes=64)
         regroup(nc.scalar.copy, g_w2[:], w2[:])
         constants()
         quantise_num(2)
         sine_stream(11)
         quantise_sin(0)
+        nc.vector.tensor_copy(out=b1f[:], in_=b1raw[:])
         layer1(0)
         sine_stream(5)
         quantise(cw[:, 3, :], sw[:, 3, :], g_w2[:])
         quantise_sin(1)
         layer1(1)
-        hidden_leaky(0)
-        quantise_hidden(0)
-        outputs(0, ((quantise_sin, 2), (layer1, 2)))
-        hidden_leaky(1)
-        quantise_hidden(1)
-        outputs(1, ((hidden_leaky, 2),))
-        quantise_hidden(2)
-        outputs(2, ())
+        hidden_all(0)
+        outputs(0, (), (lambda: quantise_sin(2), lambda: layer1(2)))
+        hidden_all(1)
+        outputs(1, (lambda: hidden_leaky(2, 0),), (lambda: hidden_leaky(2, 1),))
+        quantise_hidden(2, 0)
+        quantise_hidden(2, 1)
+        outputs(2, (), ())

@@ -28,11 +28,16 @@ def row(vec):
     return vec.rearrange("(o n) -> o n", o=1)
 
 
+def by_runs_out(grouped):
+    return grouped.rearrange("p (c i) t -> p c t i", i=4)
+
+
+def by_runs_in(planes):
+    return planes.rearrange("p t (c i) -> p c t i", i=4)
+
+
 def regroup(copy, dst, src):
-    copy(
-        out=dst.rearrange("p (c i) t -> p c t i", i=4),
-        in_=src.rearrange("p t (c i) -> p c t i", i=4),
-    )
+    copy(out=by_runs_out(dst), in_=by_runs_in(src))
 
 
 def tile_claimencoder_kernel(
@@ -134,6 +139,7 @@ def tile_claimencoder_kernel(
         sb = keep.tile([P, SLOTS], F32)
         bq = keep.tile([P, SLOTS], F32)
         b1f = keep.tile([P, 4], F32)
+        b1s = keep.tile([P, 4], F32)
 
         def quantise(codes, scales, grouped):
             nc.vector.quantize_mx(
@@ -177,9 +183,9 @@ def tile_claimencoder_kernel(
         def num_leaky(c):
             for j in range(CH // P):
                 nc.vector.tensor_tensor(
-                    out=g_c[:, j * P : (j + 1) * P, 0:3],
-                    in0=banks[(c, j)][:, 0:3, :].rearrange("p t b -> p b t"),
-                    in1=smalls[(c, j)][:].rearrange("p t b -> p b t"),
+                    out=by_runs_out(g_c[:, j * P : (j + 1) * P, 0:3]),
+                    in0=by_runs_in(banks[(c, j)][:, 0:3, :]),
+                    in1=by_runs_in(smalls[(c, j)][:]),
                     op=ALU.max,
                 )
 
@@ -235,8 +241,13 @@ def tile_claimencoder_kernel(
 
         biased = {}
 
-        def layer1(c):
+        lows = {}
+
+        def layer1(c, with_low):
             pre1 = work.tile([P, 4, CH], F32, tag="pre1")
+            if with_low:
+                low = work.tile([P, 4, CH], F32, tag="low")
+                lows[c] = low
             for m in range(4):
                 ms = slice(m * P, (m + 1) * P)
                 acc = psum.tile([P, CH], F32, tag="bank")
@@ -248,6 +259,10 @@ def tile_claimencoder_kernel(
                         start=(i == 0), stop=(i == 2),
                     )
                 nc.scalar.activation(out=pre1[:, m, :], in_=acc[:], func=ACT.Identity, bias=b1f[:, m : m + 1], scale=1.0)
+                if with_low:
+                    nc.scalar.activation(
+                        out=lows[c][:, m, :], in_=acc[:], func=ACT.Identity, bias=b1s[:, m : m + 1], scale=SLOPE
+                    )
             biased[c] = pre1
 
         grouped_h = {}
@@ -255,22 +270,43 @@ def tile_claimencoder_kernel(
 
         HALF = CH // 2
 
+        def halves(half):
+            return slice(half * HALF, (half + 1) * HALF)
+
+        def new_grouped_h(c):
+            g_h = work.tile([P, CH, 4], BF16, tag="g_h", align_bytes=64)
+            grouped_h[c] = g_h
+
         def hidden_leaky(c, half):
             if half == 0:
-                g_h = work.tile([P, CH, 4], BF16, tag="g_h", align_bytes=64)
-                grouped_h[c] = g_h
-            hs = slice(half * HALF, (half + 1) * HALF)
-            by_claim = biased[c][:].rearrange("p t b -> p b t")[:, hs, :]
-            nc.vector.scalar_tensor_tensor(
-                out=grouped_h[c][:, hs, :], in0=by_claim, scalar=SLOPE, in1=by_claim, op0=ALU.mult, op1=ALU.max
+                new_grouped_h(c)
+            hs = halves(half)
+            nc.vector.tensor_tensor(
+                out=by_runs_out(grouped_h[c][:, hs, :]),
+                in0=by_runs_in(biased[c][:, :, hs]),
+                in1=by_runs_in(lows[c][:, :, hs]),
+                op=ALU.max,
             )
+
+        def hidden_leaky_planes(c):
+            hp = work.tile([P, 4, CH], BF16, tag="hp")
+            new_grouped_h(c)
+            for half in range(2):
+                hs = halves(half)
+                nc.vector.scalar_tensor_tensor(
+                    out=hp[:, :, hs], in0=biased[c][:, :, hs], scalar=SLOPE, in1=biased[c][:, :, hs],
+                    op0=ALU.mult, op1=ALU.max,
+                )
+            for half in range(2):
+                hs = halves(half)
+                regroup(nc.vector.tensor_copy, grouped_h[c][:, hs, :], hp[:, :, hs])
 
         def quantise_hidden(c, half):
             if half == 0:
                 ch = work.tile([P, CH], U32, tag="ch", align_bytes=64)
                 sh = work.tile([P, CH], U8, tag="sh", align_bytes=64)
                 hidden[c] = (ch, sh)
-            hs = slice(half * HALF, (half + 1) * HALF)
+            hs = halves(half)
             quantise(hidden[c][0][:, hs], hidden[c][1][:, hs], grouped_h[c][:, hs, :])
             layer2(c, 2 * half)
             layer2(c, 2 * half + 1)
@@ -318,12 +354,6 @@ def tile_claimencoder_kernel(
                 step()
             finish(c, 3)
 
-        def hidden_all(c):
-            hidden_leaky(c, 0)
-            hidden_leaky(c, 1)
-            quantise_hidden(c, 0)
-            quantise_hidden(c, 1)
-
         num_products(0)
         num_products(1)
         g_w1 = keep.tile([P, H, 4], BF16, align_bytes=64)
@@ -347,14 +377,20 @@ def tile_claimencoder_kernel(
         sine_stream(11)
         quantise_sin(0)
         nc.vector.tensor_copy(out=b1f[:], in_=b1raw[:])
-        layer1(0)
+        nc.vector.tensor_scalar(out=b1s[:], in0=b1raw[:], scalar1=SLOPE, scalar2=None, op0=ALU.mult)
+        layer1(0, False)
         sine_stream(5)
         quantise(cw[:, 3, :], sw[:, 3, :], g_w2[:])
         quantise_sin(1)
-        layer1(1)
-        hidden_all(0)
-        outputs(0, (), (lambda: quantise_sin(2), lambda: layer1(2)))
-        hidden_all(1)
+        layer1(1, True)
+        hidden_leaky_planes(0)
+        quantise_hidden(0, 0)
+        quantise_hidden(0, 1)
+        outputs(0, (), (lambda: quantise_sin(2), lambda: layer1(2, True)))
+        hidden_leaky(1, 0)
+        hidden_leaky(1, 1)
+        quantise_hidden(1, 0)
+        quantise_hidden(1, 1)
         outputs(1, (lambda: hidden_leaky(2, 0),), (lambda: hidden_leaky(2, 1),))
         quantise_hidden(2, 0)
         quantise_hidden(2, 1)

@@ -56,11 +56,11 @@ def tile_claimencoder_kernel(
         psum = ctx.enter_context(tc.psum_pool(name="psum", bufs=8))
         ctx.enter_context(tc.manual_schedule())
 
-        w1s = keep.tile([P, SLOTS, H], BF16)
-        nc.gpsimd.dma_start(out=w1s[:], in_=W1[0:640, :].rearrange("(p s) n -> p s n", s=SLOTS))
-
         def load(dst, src):
             nc.sync.dma_start(out=dst, in_=src)
+
+        w1s = keep.tile([P, SLOTS, H], BF16)
+        load(w1s[:], W1[0:640, :].rearrange("(p s) n -> p s n", s=SLOTS))
 
         warm = keep.tile([P, 1], F32)
         nc.vector.memset(warm[:], 0.0)
@@ -74,13 +74,8 @@ def tile_claimencoder_kernel(
         rows_num = keep.tile([P, B], BF16)
         nc.vector.memset(rows_num[:], 0.0)
         nc.vector.memset(rows_num[96:128, :], 1.0)
-        nc.gpsimd.dma_start(out=rows_num[64:65, :], in_=row(wait_dst))
-        load(rows_num[0:1, :], row(time_s))
-        load(rows_num[32:33, :], row(wait_src))
-        w1n = keep.tile([P, 3, H], BF16)
-        nc.gpsimd.dma_start(out=w1n[:], in_=W1[640:1024, :].rearrange("(t p) n -> p t n", p=P))
-        w2 = keep.tile([P, 4, H], BF16)
-        nc.gpsimd.dma_start(out=w2[:], in_=W2.rearrange("(t p) n -> p t n", p=P))
+        for t, scal in enumerate((time_s, wait_src, wait_dst)):
+            load(rows_num[32 * t : 32 * t + 1, :], row(scal))
 
         g_c = keep.tile([P, CH, 4], BF16, align_bytes=64)
         nc.vector.memset(g_c[:], 0.0)
@@ -107,28 +102,32 @@ def tile_claimencoder_kernel(
             load(pw[lo + 16 : lo + 32, :], w_cos.rearrange("(l s) -> l s", s=SLOTS))
             load(pb[lo : lo + 16, :], b_sin.rearrange("(l s) -> l s", s=SLOTS))
             load(pb[lo + 16 : lo + 32, :], b_cos.rearrange("(l s) -> l s", s=SLOTS))
-        b1raw = keep.tile([P, 4], BF16)
-        with nc.allow_non_contiguous_dma(reason="512 bias values, one per partition and output tile"):
-            load(b1raw[:], b1.rearrange("(m p) -> p m", p=P))
-        b2bc = keep.tile([P, H], BF16)
-        load(b2bc[:], b2.partition_broadcast(P))
 
         sel = keep.tile([P, P], BF16)
         nc.vector.memset(sel[:], 0.0)
         for g in range(4):
             nc.vector.memset(sel[32 * g : 32 * g + 32, 32 * g : 32 * g + 32], 1.0)
+        g_wb = keep.tile([P, H, 4], BF16, align_bytes=64)
+        nc.vector.memset(g_wb[:], 0.0)
         g_wc = keep.tile([P, H, 4], BF16, align_bytes=64)
         nc.vector.memset(g_wc[:], 0.0)
+        g_b0 = keep.tile([P, CH, 4], BF16, align_bytes=64)
+        nc.vector.memset(g_b0[:], 0.0)
+        g_b1 = keep.tile([P, CH, 4], BF16, align_bytes=64)
+        nc.vector.memset(g_b1[:], 0.0)
+        g_bs = (g_b0, g_b1, g_b0)
 
         lane = keep.tile([P, 1], I32)
         nc.gpsimd.iota(lane[:], pattern=[[0, 1]], base=0, channel_multiplier=1)
-        g_wb = keep.tile([P, H, 4], BF16, align_bytes=64)
-        nc.gpsimd.memset(g_wb[:].rearrange("p n t -> p (n t)").bitcast(F32), 0.0)
-        g_bs = []
-        for c in range(NCH):
-            g_b = keep.tile([P, CH, 4], BF16, name="g_b%d" % c, align_bytes=64)
-            nc.gpsimd.memset(g_b[:].rearrange("p n t -> p (n t)").bitcast(F32), 0.0)
-            g_bs.append(g_b)
+        w1n = keep.tile([P, 3, H], BF16)
+        nc.gpsimd.dma_start(out=w1n[:], in_=W1[640:1024, :].rearrange("(t p) n -> p t n", p=P))
+        w2 = keep.tile([P, 4, H], BF16)
+        nc.gpsimd.dma_start(out=w2[:], in_=W2.rearrange("(t p) n -> p t n", p=P))
+        b1raw = keep.tile([P, 4], BF16)
+        with nc.allow_non_contiguous_dma(reason="512 bias values, one per partition and output tile"):
+            nc.gpsimd.dma_start(out=b1raw[:], in_=b1.rearrange("(m p) -> p m", p=P))
+        b2bc = keep.tile([P, H], BF16)
+        nc.gpsimd.dma_start(out=b2bc[:], in_=b2.partition_broadcast(P))
 
         cw = keep.tile([P, 4, H], U32, align_bytes=64)
         sw = keep.tile([P, 4, H], U8, align_bytes=64)
@@ -358,23 +357,24 @@ def tile_claimencoder_kernel(
         num_products(1)
         g_w1 = keep.tile([P, H, 4], BF16, align_bytes=64)
         regroup(nc.vector.tensor_copy, g_w1[:], w1s[:, 0:4, :])
+        nc.scalar.copy(out=g_wb[:, :, 0], in_=w1s[:, 4, :])
         num_leaky(0)
         quantise(cw[:, 0, :], sw[:, 0, :], g_w1[:])
         quantise_num(0)
         num_leaky(1)
-        regroup(nc.scalar.copy, g_wc[:, :, 0:3], w1n[:])
         num_products(2)
-        nc.scalar.copy(out=g_wb[:, :, 0], in_=w1s[:, 4, :])
         spread_points()
-        quantise(cw[:, 2, :], sw[:, 2, :], g_wc[:])
+        quantise(cw[:, 1, :], sw[:, 1, :], g_wb[:])
         quantise_num(1)
         num_leaky(2)
-        quantise(cw[:, 1, :], sw[:, 1, :], g_wb[:])
+        regroup(nc.scalar.copy, g_wc[:, :, 0:3], w1n[:])
         g_w2 = keep.tile([P, H, 4], BF16, align_bytes=64)
         regroup(nc.scalar.copy, g_w2[:], w2[:])
         constants()
         quantise_num(2)
-        sine_stream(11)
+        sine_stream(6)
+        quantise(cw[:, 2, :], sw[:, 2, :], g_wc[:])
+        sine_stream(5)
         quantise_sin(0)
         nc.vector.tensor_copy(out=b1f[:], in_=b1raw[:])
         nc.vector.tensor_scalar(out=b1s[:], in0=b1raw[:], scalar1=SLOPE, scalar2=None, op0=ALU.mult)

@@ -20,6 +20,7 @@ H = 512
 SLOTS = 5
 TWO_PI = 2.0 * math.pi
 SLOPE = 0.01
+TWO_ONES = 0x3F803F80
 
 FLOPS = 2 * B * 1024 * H + 2 * B * H * H
 
@@ -59,6 +60,9 @@ def tile_claimencoder_kernel(
         def load(dst, src):
             nc.sync.dma_start(out=dst, in_=src)
 
+        def fill(bf16_view, word):
+            nc.vector.memset(bf16_view.bitcast(I32), word)
+
         w1s = keep.tile([P, SLOTS, H], BF16)
         load(w1s[:], W1[0:640, :].rearrange("(p s) n -> p s n", s=SLOTS))
 
@@ -67,20 +71,20 @@ def tile_claimencoder_kernel(
         warmed = keep.tile([P, 1], F32)
         nc.scalar.activation(out=warmed[:], in_=warm[:], func=ACT.Sin)
         num_wb = keep.tile([P, 3, P], BF16)
-        nc.vector.memset(num_wb[:], 0.0)
+        fill(num_wb[:].rearrange("p t n -> p (t n)"), 0)
         for t, (w_t, b_t) in enumerate(((t_w, t_b), (ws_w, ws_b), (wd_w, wd_b))):
             load(num_wb[32 * t : 32 * t + 1, t, :], row(w_t))
             load(num_wb[96:97, t, :], row(b_t))
         rows_num = keep.tile([P, B], BF16)
-        nc.vector.memset(rows_num[:], 0.0)
-        nc.vector.memset(rows_num[96:128, :], 1.0)
+        fill(rows_num[:], 0)
+        fill(rows_num[96:128, :], TWO_ONES)
         for t, scal in enumerate((time_s, wait_src, wait_dst)):
             load(rows_num[32 * t : 32 * t + 1, :], row(scal))
 
         g_c = keep.tile([P, CH, 4], BF16, align_bytes=64)
-        nc.vector.memset(g_c[:], 0.0)
+        fill(g_c[:].rearrange("p n t -> p (n t)"), 0)
         rows_xy = keep.tile([P, 2 * B], BF16)
-        nc.vector.memset(rows_xy[:], 0.0)
+        fill(rows_xy[:], 0)
         flat_s = src_xy.rearrange("b c -> (b c)")
         flat_d = dst_xy.rearrange("b c -> (b c)")
         load(rows_xy[0:1, :], row(flat_s))
@@ -104,17 +108,17 @@ def tile_claimencoder_kernel(
             load(pb[lo + 16 : lo + 32, :], b_cos.rearrange("(l s) -> l s", s=SLOTS))
 
         sel = keep.tile([P, P], BF16)
-        nc.vector.memset(sel[:], 0.0)
+        fill(sel[:], 0)
         for g in range(4):
-            nc.vector.memset(sel[32 * g : 32 * g + 32, 32 * g : 32 * g + 32], 1.0)
+            fill(sel[32 * g : 32 * g + 32, 32 * g : 32 * g + 32], TWO_ONES)
         g_wb = keep.tile([P, H, 4], BF16, align_bytes=64)
-        nc.vector.memset(g_wb[:], 0.0)
+        fill(g_wb[:].rearrange("p n t -> p (n t)"), 0)
         g_wc = keep.tile([P, H, 4], BF16, align_bytes=64)
-        nc.vector.memset(g_wc[:], 0.0)
+        fill(g_wc[:].rearrange("p n t -> p (n t)"), 0)
         g_b0 = keep.tile([P, CH, 4], BF16, align_bytes=64)
-        nc.vector.memset(g_b0[:], 0.0)
+        fill(g_b0[:].rearrange("p n t -> p (n t)"), 0)
         g_b1 = keep.tile([P, CH, 4], BF16, align_bytes=64)
-        nc.vector.memset(g_b1[:], 0.0)
+        fill(g_b1[:].rearrange("p n t -> p (n t)"), 0)
         g_bs = (g_b0, g_b1, g_b0)
 
         lane = keep.tile([P, 1], I32)

@@ -64,7 +64,7 @@ def tile_claimencoder_kernel(
             nc.vector.memset(bf16_view.bitcast(I32), word)
 
         w1s = keep.tile([P, SLOTS, H], BF16)
-        load(w1s[:], W1[0:640, :].rearrange("(p s) n -> p s n", s=SLOTS))
+        nc.gpsimd.dma_start(out=w1s[:], in_=W1[0:640, :].rearrange("(p s) n -> p s n", s=SLOTS))
 
         warm = keep.tile([P, 1], F32)
         nc.vector.memset(warm[:], 0.0)
@@ -72,25 +72,27 @@ def tile_claimencoder_kernel(
         nc.scalar.activation(out=warmed[:], in_=warm[:], func=ACT.Sin)
         num_wb = keep.tile([P, 3, P], BF16)
         fill(num_wb[:].rearrange("p t n -> p (t n)"), 0)
-        for t, (w_t, b_t) in enumerate(((t_w, t_b), (ws_w, ws_b), (wd_w, wd_b))):
-            load(num_wb[32 * t : 32 * t + 1, t, :], row(w_t))
-            load(num_wb[96:97, t, :], row(b_t))
-        rows_num = keep.tile([P, B], BF16)
-        fill(rows_num[:], 0)
-        fill(rows_num[96:128, :], TWO_ONES)
+        rows = keep.tile([P, 2 * B], BF16)
+        fill(rows[:, 0:B], TWO_ONES)
+        fill(rows[:, B : 2 * B], TWO_ONES)
         for t, scal in enumerate((time_s, wait_src, wait_dst)):
-            load(rows_num[32 * t : 32 * t + 1, :], row(scal))
+            load(rows[1 + t : 2 + t, 0:B], row(scal))
+        for t, w_t in enumerate((t_w, ws_w, wd_w)):
+            load(num_wb[1 + t : 2 + t, t, :], row(w_t))
+        load(num_wb[4:5, 0, :], row(t_b))
+        load(num_wb[4:5, 1, :], row(ws_b))
+        nc.gpsimd.dma_start(out=num_wb[4:5, 2, :], in_=row(wd_b))
+        w1n = keep.tile([P, 3, H], BF16)
+        nc.gpsimd.dma_start(out=w1n[:], in_=W1[640:1024, :].rearrange("(t p) n -> p t n", p=P))
 
         g_c = keep.tile([P, CH, 4], BF16, align_bytes=64)
         fill(g_c[:].rearrange("p n t -> p (n t)"), 0)
-        rows_xy = keep.tile([P, 2 * B], BF16)
-        fill(rows_xy[:], 0)
         flat_s = src_xy.rearrange("b c -> (b c)")
         flat_d = dst_xy.rearrange("b c -> (b c)")
-        load(rows_xy[0:1, :], row(flat_s))
-        load(rows_xy[32:33, 0 : 2 * B - 1], row(flat_s[1 : 2 * B]))
-        load(rows_xy[64:65, :], row(flat_d))
-        load(rows_xy[96:97, 0 : 2 * B - 1], row(flat_d[1 : 2 * B]))
+        load(rows[0:1, :], row(flat_s))
+        load(rows[32:33, 0 : 2 * B - 1], row(flat_s[1 : 2 * B]))
+        load(rows[64:65, :], row(flat_d))
+        load(rows[96:97, 0 : 2 * B - 1], row(flat_d[1 : 2 * B]))
 
         pw = keep.tile([P, SLOTS], BF16)
         pb = keep.tile([P, SLOTS], BF16)
@@ -110,21 +112,16 @@ def tile_claimencoder_kernel(
         sel = keep.tile([P, P], BF16)
         fill(sel[:], 0)
         for g in range(4):
-            fill(sel[32 * g : 32 * g + 32, 32 * g : 32 * g + 32], TWO_ONES)
+            fill(sel[32 * g : 32 * g + 1, 32 * g : 32 * g + 32], TWO_ONES)
         g_wb = keep.tile([P, H, 4], BF16, align_bytes=64)
         fill(g_wb[:].rearrange("p n t -> p (n t)"), 0)
         g_wc = keep.tile([P, H, 4], BF16, align_bytes=64)
         fill(g_wc[:].rearrange("p n t -> p (n t)"), 0)
         g_b0 = keep.tile([P, CH, 4], BF16, align_bytes=64)
-        fill(g_b0[:].rearrange("p n t -> p (n t)"), 0)
         g_b1 = keep.tile([P, CH, 4], BF16, align_bytes=64)
-        fill(g_b1[:].rearrange("p n t -> p (n t)"), 0)
         g_bs = (g_b0, g_b1, g_b0)
 
         lane = keep.tile([P, 1], I32)
-        nc.gpsimd.iota(lane[:], pattern=[[0, 1]], base=0, channel_multiplier=1)
-        w1n = keep.tile([P, 3, H], BF16)
-        nc.gpsimd.dma_start(out=w1n[:], in_=W1[640:1024, :].rearrange("(t p) n -> p t n", p=P))
         w2 = keep.tile([P, 4, H], BF16)
         nc.gpsimd.dma_start(out=w2[:], in_=W2.rearrange("(t p) n -> p t n", p=P))
         b1raw = keep.tile([P, 4], BF16)
@@ -132,6 +129,9 @@ def tile_claimencoder_kernel(
             nc.gpsimd.dma_start(out=b1raw[:], in_=b1.rearrange("(m p) -> p m", p=P))
         b2bc = keep.tile([P, H], BF16)
         nc.gpsimd.dma_start(out=b2bc[:], in_=b2.partition_broadcast(P))
+        nc.gpsimd.iota(lane[:], pattern=[[0, 1]], base=0, channel_multiplier=1)
+        for g_b in (g_b0, g_b1):
+            nc.gpsimd.memset(g_b[:].rearrange("p n t -> p (n t)").bitcast(I32), 0)
 
         cw = keep.tile([P, 4, H], U32, align_bytes=64)
         sw = keep.tile([P, 4, H], U8, align_bytes=64)
@@ -159,7 +159,7 @@ def tile_claimencoder_kernel(
             nc.vector.tensor_scalar(out=bq[:], in0=sb[:], scalar1=1.0 / TWO_PI, scalar2=None, op0=ALU.mult)
 
         def spread_points():
-            pairs = rows_xy[:].rearrange("p (b c) -> p b c", c=2)
+            pairs = rows[:].rearrange("p (b c) -> p b c", c=2)
             for c in range(NCH):
                 xps = psum.tile([P, CH], F32, tag="bank")
                 nc.tensor.matmul(
@@ -176,7 +176,7 @@ def tile_claimencoder_kernel(
                 lo = c * CH + j * P
                 for t in range(3):
                     nc.tensor.matmul(
-                        out=vps[:, t, :], lhsT=num_wb[:, t, :], rhs=rows_num[:, lo : lo + P], start=True, stop=True
+                        out=vps[:, t, :], lhsT=num_wb[:, t, :], rhs=rows[:, lo : lo + P], start=True, stop=True
                     )
                 small = work.tile([P, 3, P], F32, tag="small", bufs=8)
                 nc.scalar.activation(out=small[:], in_=vps[:, 0:3, :], func=ACT.Copy, scale=SLOPE)
@@ -361,23 +361,24 @@ def tile_claimencoder_kernel(
         num_products(1)
         g_w1 = keep.tile([P, H, 4], BF16, align_bytes=64)
         regroup(nc.vector.tensor_copy, g_w1[:], w1s[:, 0:4, :])
-        nc.scalar.copy(out=g_wb[:, :, 0], in_=w1s[:, 4, :])
         num_leaky(0)
         quantise(cw[:, 0, :], sw[:, 0, :], g_w1[:])
+        spread_points()
+        num_products(2)
+        nc.scalar.copy(out=g_wb[:, :, 0], in_=w1s[:, 4, :])
         quantise_num(0)
         num_leaky(1)
-        num_products(2)
-        spread_points()
-        quantise(cw[:, 1, :], sw[:, 1, :], g_wb[:])
+        constants()
+        regroup(nc.vector.tensor_copy, g_wc[:, :, 0:3], w1n[:])
         quantise_num(1)
+        sine_stream(2)
         num_leaky(2)
-        regroup(nc.scalar.copy, g_wc[:, :, 0:3], w1n[:])
+        quantise(cw[:, 2, :], sw[:, 2, :], g_wc[:])
+        quantise_num(2)
         g_w2 = keep.tile([P, H, 4], BF16, align_bytes=64)
         regroup(nc.scalar.copy, g_w2[:], w2[:])
-        constants()
-        quantise_num(2)
-        sine_stream(6)
-        quantise(cw[:, 2, :], sw[:, 2, :], g_wc[:])
+        sine_stream(4)
+        quantise(cw[:, 1, :], sw[:, 1, :], g_wb[:])
         sine_stream(5)
         quantise_sin(0)
         nc.vector.tensor_copy(out=b1f[:], in_=b1raw[:])

@@ -2,6 +2,7 @@ import math
 from contextlib import ExitStack
 
 import concourse.mybir as mybir
+from concourse.masks import make_identity
 
 F32 = mybir.dt.float32
 BF16 = mybir.dt.bfloat16
@@ -15,6 +16,7 @@ ACT = mybir.ActivationFunctionType
 P = 128
 B = 1536
 CH = 512
+HALF = CH // 2
 NCH = B // CH
 H = 512
 SLOTS = 5
@@ -41,6 +43,14 @@ def regroup(copy, dst, src):
     copy(out=by_runs_out(dst), in_=by_runs_in(src))
 
 
+def chunk(c):
+    return slice(c * CH, (c + 1) * CH)
+
+
+def halves(half):
+    return slice(half * HALF, (half + 1) * HALF)
+
+
 def tile_claimencoder_kernel(
     tc,
     src_xy, dst_xy, time_s, wait_src, wait_dst,
@@ -63,6 +73,14 @@ def tile_claimencoder_kernel(
         def fill(bf16_view, word):
             nc.vector.memset(bf16_view.bitcast(I32), word)
 
+        def flat(grouped):
+            return grouped[:].rearrange("p n t -> p (n t)")
+
+        def clear_late(grouped):
+            nc.gpsimd.memset(flat(grouped).bitcast(I32), 0)
+
+        lane = keep.tile([P, 1], I32)
+        nc.gpsimd.iota(lane[:], pattern=[[0, 1]], base=0, channel_multiplier=1)
         w1s = keep.tile([P, SLOTS, H], BF16)
         nc.gpsimd.dma_start(out=w1s[:], in_=W1[0:640, :].rearrange("(p s) n -> p s n", s=SLOTS))
 
@@ -72,27 +90,23 @@ def tile_claimencoder_kernel(
         nc.scalar.activation(out=warmed[:], in_=warm[:], func=ACT.Sin)
         num_wb = keep.tile([P, 3, P], BF16)
         fill(num_wb[:].rearrange("p t n -> p (t n)"), 0)
-        rows = keep.tile([P, 2 * B], BF16)
-        fill(rows[:, 0:B], TWO_ONES)
-        fill(rows[:, B : 2 * B], TWO_ONES)
-        for t, scal in enumerate((time_s, wait_src, wait_dst)):
-            load(rows[1 + t : 2 + t, 0:B], row(scal))
+        rows_num = keep.tile([P, B], BF16)
+        fill(rows_num[:], TWO_ONES)
         for t, w_t in enumerate((t_w, ws_w, wd_w)):
             load(num_wb[1 + t : 2 + t, t, :], row(w_t))
         load(num_wb[4:5, 0, :], row(t_b))
         load(num_wb[4:5, 1, :], row(ws_b))
         nc.gpsimd.dma_start(out=num_wb[4:5, 2, :], in_=row(wd_b))
-        w1n = keep.tile([P, 3, H], BF16)
-        nc.gpsimd.dma_start(out=w1n[:], in_=W1[640:1024, :].rearrange("(t p) n -> p t n", p=P))
+        for t, scal in enumerate((time_s, wait_src, wait_dst)):
+            load(rows_num[1 + t : 2 + t, :], row(scal))
 
-        g_c = keep.tile([P, CH, 4], BF16, align_bytes=64)
-        fill(g_c[:].rearrange("p n t -> p (n t)"), 0)
+        xy = keep.tile([P, 2 * B], BF16)
         flat_s = src_xy.rearrange("b c -> (b c)")
         flat_d = dst_xy.rearrange("b c -> (b c)")
-        load(rows[0:1, :], row(flat_s))
-        load(rows[32:33, 0 : 2 * B - 1], row(flat_s[1 : 2 * B]))
-        load(rows[64:65, :], row(flat_d))
-        load(rows[96:97, 0 : 2 * B - 1], row(flat_d[1 : 2 * B]))
+        for g, points in enumerate((flat_s, flat_s[1 : 2 * B], flat_d, flat_d[1 : 2 * B])):
+            n = points.shape[0]
+            load(xy[32 * g : 32 * g + 32, 0:n], points.partition_broadcast(32))
+        xs = xy[:].rearrange("p (b c) -> p b c", c=2)[:, :, 0]
 
         pw = keep.tile([P, SLOTS], BF16)
         pb = keep.tile([P, SLOTS], BF16)
@@ -102,47 +116,53 @@ def tile_claimencoder_kernel(
             (dst_wsx, dst_bsx, dst_wcx, dst_bcx),
             (dst_wsy, dst_bsy, dst_wcy, dst_bcy),
         )
-        for g, (w_sin, b_sin, w_cos, b_cos) in enumerate(groups):
-            lo = 32 * g
-            load(pw[lo : lo + 16, :], w_sin.rearrange("(l s) -> l s", s=SLOTS))
-            load(pw[lo + 16 : lo + 32, :], w_cos.rearrange("(l s) -> l s", s=SLOTS))
-            load(pb[lo : lo + 16, :], b_sin.rearrange("(l s) -> l s", s=SLOTS))
-            load(pb[lo + 16 : lo + 32, :], b_cos.rearrange("(l s) -> l s", s=SLOTS))
+        for g, vecs in enumerate(groups):
+            queue = nc.gpsimd if g == 3 else nc.sync
+            for i, vec in enumerate(vecs):
+                dst = pb if i % 2 else pw
+                lo = 32 * g + 16 * (i // 2)
+                queue.dma_start(out=dst[lo : lo + 16, :], in_=vec.rearrange("(l s) -> l s", s=SLOTS))
 
-        sel = keep.tile([P, P], BF16)
-        fill(sel[:], 0)
-        for g in range(4):
-            fill(sel[32 * g : 32 * g + 1, 32 * g : 32 * g + 32], TWO_ONES)
+        g_c = keep.tile([P, CH, 4], BF16, align_bytes=64)
+        fill(flat(g_c), 0)
+        bit = keep.tile([P, 1], I32)
+        nc.vector.tensor_scalar(out=bit[:], in0=lane[:], scalar1=16, scalar2=None, op0=ALU.bitwise_and)
         g_wb = keep.tile([P, H, 4], BF16, align_bytes=64)
-        fill(g_wb[:].rearrange("p n t -> p (n t)"), 0)
+        fill(flat(g_wb), 0)
+        phase = keep.tile([P, 1], F32)
+        nc.vector.tensor_scalar(out=phase[:], in0=bit[:], scalar1=math.pi / 32.0, scalar2=None, op0=ALU.mult)
         g_wc = keep.tile([P, H, 4], BF16, align_bytes=64)
-        fill(g_wc[:].rearrange("p n t -> p (n t)"), 0)
-        g_b0 = keep.tile([P, CH, 4], BF16, align_bytes=64)
-        g_b1 = keep.tile([P, CH, 4], BF16, align_bytes=64)
-        g_bs = (g_b0, g_b1, g_b0)
+        fill(flat(g_wc), 0)
 
-        lane = keep.tile([P, 1], I32)
+        w1n = keep.tile([P, 3, H], BF16)
+        nc.gpsimd.dma_start(out=w1n[:], in_=W1[640:1024, :].rearrange("(t p) n -> p t n", p=P))
         w2 = keep.tile([P, 4, H], BF16)
         nc.gpsimd.dma_start(out=w2[:], in_=W2.rearrange("(t p) n -> p t n", p=P))
+        g_b0 = keep.tile([P, CH, 4], BF16, align_bytes=64)
+        clear_late(g_b0)
         b1raw = keep.tile([P, 4], BF16)
         with nc.allow_non_contiguous_dma(reason="512 bias values, one per partition and output tile"):
             nc.gpsimd.dma_start(out=b1raw[:], in_=b1.rearrange("(m p) -> p m", p=P))
         b2bc = keep.tile([P, H], BF16)
         nc.gpsimd.dma_start(out=b2bc[:], in_=b2.partition_broadcast(P))
-        nc.gpsimd.iota(lane[:], pattern=[[0, 1]], base=0, channel_multiplier=1)
-        for g_b in (g_b0, g_b1):
-            nc.gpsimd.memset(g_b[:].rearrange("p n t -> p (n t)").bitcast(I32), 0)
+        g_b1 = keep.tile([P, CH, 4], BF16, align_bytes=64)
+        clear_late(g_b1)
+        g_bs = (g_b0, g_b1, g_b0)
+        ident = keep.tile([P, P], F32)
+        make_identity(nc, ident[:])
 
         cw = keep.tile([P, 4, H], U32, align_bytes=64)
         sw = keep.tile([P, 4, H], U8, align_bytes=64)
         cf = keep.tile([P, 3, B], U32, align_bytes=64)
         sf = keep.tile([P, 3, B], U8, align_bytes=64)
-        xs = keep.tile([P, B], BF16)
         wq = keep.tile([P, SLOTS], F32)
         sb = keep.tile([P, SLOTS], F32)
         bq = keep.tile([P, SLOTS], F32)
         b1f = keep.tile([P, 4], F32)
-        b1s = keep.tile([P, 4], F32)
+        b2f = keep.tile([P, H], F32)
+        b2c = keep.tile([P, 4], F32)
+        g_w1 = keep.tile([P, H, 4], BF16, align_bytes=64)
+        g_w2 = keep.tile([P, H, 4], BF16, align_bytes=64)
 
         def quantise(codes, scales, grouped):
             nc.vector.quantize_mx(
@@ -150,22 +170,11 @@ def tile_claimencoder_kernel(
             )
 
         def constants():
-            bit = keep.tile([P, 1], I32)
-            nc.vector.tensor_scalar(out=bit[:], in0=lane[:], scalar1=16, scalar2=None, op0=ALU.bitwise_and)
-            phase = keep.tile([P, 1], F32)
-            nc.vector.tensor_scalar(out=phase[:], in0=bit[:], scalar1=math.pi / 32.0, scalar2=None, op0=ALU.mult)
             nc.vector.tensor_scalar(out=wq[:], in0=pw[:], scalar1=1.0 / TWO_PI, scalar2=None, op0=ALU.mult)
+            nc.vector.tensor_scalar(
+                out=bq[:], in0=pb[:], scalar1=phase[:, 0:1], scalar2=1.0 / TWO_PI, op0=ALU.add, op1=ALU.mult
+            )
             nc.vector.tensor_scalar(out=sb[:], in0=pb[:], scalar1=phase[:, 0:1], scalar2=None, op0=ALU.add)
-            nc.vector.tensor_scalar(out=bq[:], in0=sb[:], scalar1=1.0 / TWO_PI, scalar2=None, op0=ALU.mult)
-
-        def spread_points():
-            pairs = rows[:].rearrange("p (b c) -> p b c", c=2)
-            for c in range(NCH):
-                xps = psum.tile([P, CH], F32, tag="bank")
-                nc.tensor.matmul(
-                    out=xps[:], lhsT=sel[:], rhs=pairs[:, c * CH : (c + 1) * CH, 0], start=True, stop=True
-                )
-                nc.scalar.copy(out=xs[:, c * CH : (c + 1) * CH], in_=xps[:])
 
         banks = {}
         smalls = {}
@@ -176,7 +185,7 @@ def tile_claimencoder_kernel(
                 lo = c * CH + j * P
                 for t in range(3):
                     nc.tensor.matmul(
-                        out=vps[:, t, :], lhsT=num_wb[:, t, :], rhs=rows[:, lo : lo + P], start=True, stop=True
+                        out=vps[:, t, :], lhsT=num_wb[:, t, :], rhs=rows_num[:, lo : lo + P], start=True, stop=True
                     )
                 small = work.tile([P, 3, P], F32, tag="small", bufs=8)
                 nc.scalar.activation(out=small[:], in_=vps[:, 0:3, :], func=ACT.Copy, scale=SLOPE)
@@ -192,39 +201,38 @@ def tile_claimencoder_kernel(
                     op=ALU.max,
                 )
 
-        def chunk(c):
-            return slice(c * CH, (c + 1) * CH)
-
         def quantise_num(c):
             quantise(cf[:, 2, chunk(c)], sf[:, 2, chunk(c)], g_c[:])
 
         turn_tiles = {}
+        frac_tiles = {}
         plane_tiles = {}
         grouped_a = {}
 
-        def count_turns(c, s):
-            turns = work.tile([P, CH], I32, tag="turns", bufs=4)
+        def turns(c, s):
+            turn = work.tile([P, CH], I32, tag="turn", bufs=4)
             nc.vector.tensor_scalar(
-                out=turns[:], in0=xs[:, chunk(c)], scalar1=wq[:, s : s + 1], scalar2=bq[:, s : s + 1],
+                out=turn[:], in0=xs[:, chunk(c)], scalar1=wq[:, s : s + 1], scalar2=bq[:, s : s + 1],
                 op0=ALU.mult, op1=ALU.add,
             )
-            turn_tiles[(c, s)] = turns
+            turn_tiles[(c, s)] = turn
 
-        def sine(c, s):
-            frac = work.tile([P, CH], F32, tag="frac", bufs=6)
+        def fracs(c, s):
+            frac = work.tile([P, CH], F32, tag="frac", bufs=8)
             nc.vector.scalar_tensor_tensor(
                 out=frac[:], in0=xs[:, chunk(c)], scalar=wq[:, s : s + 1], in1=turn_tiles[(c, s)][:],
                 op0=ALU.mult, op1=ALU.subtract,
             )
+            frac_tiles[(c, s)] = frac
+
+        def sines(c, s):
             if s == 0:
                 planes = work.tile([P, 4, CH], BF16, tag="planes")
                 plane_tiles[c] = planes
             dst = plane_tiles[c][:, s, :] if s < 4 else g_bs[c][:, :, 0]
-            nc.scalar.activation(out=dst, in_=frac[:], func=ACT.Sin, bias=sb[:, s : s + 1], scale=TWO_PI)
-            if s == 4:
-                g_a = work.tile([P, CH, 4], BF16, tag="g_a", bufs=3, align_bytes=64)
-                regroup(nc.scalar.copy, g_a[:], plane_tiles[c][:])
-                grouped_a[c] = g_a
+            nc.scalar.activation(
+                out=dst, in_=frac_tiles[(c, s)][:], func=ACT.Sin, bias=sb[:, s : s + 1], scale=TWO_PI
+            )
 
         slots = [(c, s) for c in range(NCH) for s in range(SLOTS)]
         done = []
@@ -233,106 +241,80 @@ def tile_claimencoder_kernel(
             for step in range(steps):
                 i = len(done)
                 if i < len(slots):
-                    count_turns(slots[i][0], slots[i][1])
+                    turns(slots[i][0], slots[i][1])
                 if 0 < i <= len(slots):
-                    sine(slots[i - 1][0], slots[i - 1][1])
+                    fracs(slots[i - 1][0], slots[i - 1][1])
+                    sines(slots[i - 1][0], slots[i - 1][1])
                 done.append(i)
 
+        def group_sines(c, copy):
+            g_a = work.tile([P, CH, 4], BF16, tag="g_a", align_bytes=64)
+            regroup(copy, g_a[:], plane_tiles[c][:])
+            grouped_a[c] = g_a
+
         def quantise_sin(c):
-            quantise(cf[:, 0, chunk(c)], sf[:, 0, chunk(c)], grouped_a[c][:])
             quantise(cf[:, 1, chunk(c)], sf[:, 1, chunk(c)], g_bs[c][:])
+            quantise(cf[:, 0, chunk(c)], sf[:, 0, chunk(c)], grouped_a[c][:])
 
         biased = {}
 
-        lows = {}
-
-        def layer1(c, with_low):
-            pre1 = work.tile([P, 4, CH], F32, tag="pre1")
-            if with_low:
-                low = work.tile([P, 4, CH], F32, tag="low")
-                lows[c] = low
+        def layer1(c, half, width=1):
+            pre1 = work.tile([P, 4, width * HALF], F32, tag="pre1", bufs=3)
+            lo = c * CH + half * HALF
+            cols = slice(lo, lo + width * HALF)
             for m in range(4):
                 ms = slice(m * P, (m + 1) * P)
-                acc = psum.tile([P, CH], F32, tag="bank")
-                for i in range(3):
+                acc = psum.tile([P, width * HALF], F32, tag="bank")
+                for n, i in enumerate((2, 1, 0)):
                     nc.tensor.matmul_mx(
                         out=acc[:],
                         lhsT=cw[:, i, ms].bitcast(FP8X4), lhsT_scale=sw[:, i, ms],
-                        rhs=cf[:, i, chunk(c)].bitcast(FP8X4), rhs_scale=sf[:, i, chunk(c)],
-                        start=(i == 0), stop=(i == 2),
+                        rhs=cf[:, i, cols].bitcast(FP8X4), rhs_scale=sf[:, i, cols],
+                        start=(n == 0), stop=(n == 2),
                     )
                 nc.scalar.activation(out=pre1[:, m, :], in_=acc[:], func=ACT.Identity, bias=b1f[:, m : m + 1], scale=1.0)
-                if with_low:
-                    nc.scalar.activation(
-                        out=lows[c][:, m, :], in_=acc[:], func=ACT.Identity, bias=b1s[:, m : m + 1], scale=SLOPE
-                    )
-            biased[c] = pre1
+            for w in range(width):
+                biased[(c, half + w)] = pre1[:, :, w * HALF : (w + 1) * HALF]
 
         grouped_h = {}
         hidden = {}
 
-        HALF = CH // 2
-
-        def halves(half):
-            return slice(half * HALF, (half + 1) * HALF)
-
-        def new_grouped_h(c):
-            g_h = work.tile([P, CH, 4], BF16, tag="g_h", align_bytes=64)
-            grouped_h[c] = g_h
-
         def hidden_leaky(c, half):
-            if half == 0:
-                new_grouped_h(c)
-            hs = halves(half)
-            nc.vector.tensor_tensor(
-                out=by_runs_out(grouped_h[c][:, hs, :]),
-                in0=by_runs_in(biased[c][:, :, hs]),
-                in1=by_runs_in(lows[c][:, :, hs]),
-                op=ALU.max,
-            )
-
-        def hidden_leaky_planes(c):
-            hp = work.tile([P, 4, CH], BF16, tag="hp")
-            new_grouped_h(c)
-            for half in range(2):
-                hs = halves(half)
-                nc.vector.scalar_tensor_tensor(
-                    out=hp[:, :, hs], in0=biased[c][:, :, hs], scalar=SLOPE, in1=biased[c][:, :, hs],
-                    op0=ALU.mult, op1=ALU.max,
-                )
-            for half in range(2):
-                hs = halves(half)
-                regroup(nc.vector.tensor_copy, grouped_h[c][:, hs, :], hp[:, :, hs])
+            g_h = work.tile([P, HALF, 4], BF16, tag="g_h", bufs=4, align_bytes=64)
+            grouped_h[(c, half)] = g_h
+            v = biased[(c, half)].rearrange("p m n -> p n m")
+            nc.vector.scalar_tensor_tensor(out=g_h[:], in0=v, scalar=SLOPE, in1=v, op0=ALU.mult, op1=ALU.max)
 
         def quantise_hidden(c, half):
-            if half == 0:
-                ch = work.tile([P, CH], U32, tag="ch", align_bytes=64)
-                sh = work.tile([P, CH], U8, tag="sh", align_bytes=64)
-                hidden[c] = (ch, sh)
-            hs = halves(half)
-            quantise(hidden[c][0][:, hs], hidden[c][1][:, hs], grouped_h[c][:, hs, :])
-            layer2(c, 2 * half)
-            layer2(c, 2 * half + 1)
+            ch = work.tile([P, HALF], U32, tag="ch", bufs=4, align_bytes=64)
+            sh = work.tile([P, HALF], U8, tag="sh", bufs=4, align_bytes=64)
+            hidden[(c, half)] = (ch, sh)
+            quantise(ch[:], sh[:], grouped_h[(c, half)][:])
 
         sums = {}
         pres = {}
 
-        def layer2(c, j):
-            ch, sh = hidden[c]
-            js = slice(j * P, (j + 1) * P)
-            acc = psum.tile([P, H], F32, tag="bank")
-            nc.tensor.matmul_mx(
-                out=acc[:],
-                lhsT=ch[:, js].bitcast(FP8X4), lhsT_scale=sh[:, js],
-                rhs=cw[:, 3, :].bitcast(FP8X4), rhs_scale=sw[:, 3, :],
-                start=True, stop=True,
-            )
-            sums[(c, j)] = acc
+        def layer2(c, half):
+            ch, sh = hidden[(c, half)]
+            for i in range(2):
+                js = slice(i * P, (i + 1) * P)
+                acc = psum.tile([P, H], F32, tag="bank")
+                nc.tensor.matmul_mx(
+                    out=acc[:],
+                    lhsT=ch[:, js].bitcast(FP8X4), lhsT_scale=sh[:, js],
+                    rhs=cw[:, 3, :].bitcast(FP8X4), rhs_scale=sw[:, 3, :],
+                    start=True, stop=True,
+                )
+                sums[(c, 2 * half + i)] = acc
 
         def add_bias(c, j):
             pre = work.tile([P, H], F32, tag="pre", bufs=4)
             nc.vector.tensor_tensor(out=pre[:], in0=sums[(c, j)][:], in1=b2bc[:], op=ALU.add)
             pres[(c, j)] = pre
+
+        def store(c, j, res):
+            lo = c * CH + j * P
+            nc.sync.dma_start(out=out[lo : lo + P, :], in_=res[:])
 
         def finish(c, j):
             res = work.tile([P, H], F32, tag="res", bufs=4)
@@ -340,63 +322,134 @@ def tile_claimencoder_kernel(
             nc.vector.scalar_tensor_tensor(
                 out=res[:], in0=pre[:], scalar=SLOPE, in1=pre[:], op0=ALU.mult, op1=ALU.max
             )
-            lo = c * CH + j * P
-            nc.sync.dma_start(out=out[lo : lo + P, :], in_=res[:])
+            store(c, j, res)
 
-        def outputs(c, before_third, before_last):
-            add_bias(c, 0)
-            add_bias(c, 1)
-            finish(c, 0)
-            add_bias(c, 2)
-            finish(c, 1)
-            add_bias(c, 3)
-            for step in before_third:
-                step()
-            finish(c, 2)
-            for step in before_last:
-                step()
-            finish(c, 3)
+        def bias_columns():
+            nc.scalar.copy(out=b2f[:], in_=b2bc[:])
+            bps = psum.tile([P, 4, P], F32, tag="bank")
+            for m in range(4):
+                nc.tensor.transpose(out=bps[:, m, :], in_=b2f[:, m * P : (m + 1) * P], identity=ident[:])
+            nc.scalar.copy(out=b2c[:], in_=bps[:, :, 0])
+
+        upright = {}
+        turned = {}
+        turned_lows = {}
+
+        def turned_layer2(c, half):
+            ch, sh = hidden[(c, half)]
+            vt = work.tile([P, 4, HALF], F32, tag="vt")
+            upright[(c, half)] = vt
+            for pair in range(2):
+                acc = psum.tile([P, 2, HALF], F32, tag="bank")
+                for i in range(2):
+                    m = 2 * pair + i
+                    ms = slice(m * P, (m + 1) * P)
+                    nc.tensor.matmul_mx(
+                        out=acc[:, i, :],
+                        lhsT=cw[:, 3, ms].bitcast(FP8X4), lhsT_scale=sw[:, 3, ms],
+                        rhs=ch[:].bitcast(FP8X4), rhs_scale=sh[:],
+                        start=True, stop=True,
+                    )
+                for i in range(2):
+                    m = 2 * pair + i
+                    nc.scalar.activation(
+                        out=vt[:, m, :], in_=acc[:, i, :], func=ACT.Identity, bias=b2c[:, m : m + 1], scale=1.0
+                    )
+
+        def turn_back(c, half):
+            for i in range(2):
+                j = 2 * half + i
+                tps = psum.tile([P, H], F32, tag="bank")
+                for m in range(4):
+                    nc.tensor.transpose(
+                        out=tps[:, m * P : (m + 1) * P],
+                        in_=upright[(c, half)][:, m, i * P : (i + 1) * P], identity=ident[:],
+                    )
+                turned[(c, j)] = tps
+                tlow = work.tile([P, H], F32, tag="tlow", bufs=4)
+                nc.scalar.activation(out=tlow[:], in_=tps[:], func=ACT.Copy, scale=SLOPE)
+                turned_lows[(c, j)] = tlow
+
+        def finish_turned(c, j):
+            res = work.tile([P, H], F32, tag="res", bufs=4)
+            nc.vector.tensor_tensor(out=res[:], in0=turned[(c, j)][:], in1=turned_lows[(c, j)][:], op=ALU.max)
+            store(c, j, res)
 
         num_products(0)
         num_products(1)
-        g_w1 = keep.tile([P, H, 4], BF16, align_bytes=64)
         regroup(nc.vector.tensor_copy, g_w1[:], w1s[:, 0:4, :])
         num_leaky(0)
         quantise(cw[:, 0, :], sw[:, 0, :], g_w1[:])
-        spread_points()
         num_products(2)
         nc.scalar.copy(out=g_wb[:, :, 0], in_=w1s[:, 4, :])
         quantise_num(0)
         num_leaky(1)
         constants()
-        regroup(nc.vector.tensor_copy, g_wc[:, :, 0:3], w1n[:])
+        sine_stream(3)
         quantise_num(1)
-        sine_stream(2)
+        regroup(nc.scalar.copy, g_wc[:, :, 0:3], w1n[:])
+        sine_stream(3)
+        group_sines(0, nc.scalar.copy)
         num_leaky(2)
-        quantise(cw[:, 2, :], sw[:, 2, :], g_wc[:])
-        quantise_num(2)
-        g_w2 = keep.tile([P, H, 4], BF16, align_bytes=64)
-        regroup(nc.scalar.copy, g_w2[:], w2[:])
-        sine_stream(4)
         quantise(cw[:, 1, :], sw[:, 1, :], g_wb[:])
-        sine_stream(5)
-        quantise_sin(0)
+        sine_stream(2)
+        quantise_num(2)
+        regroup(nc.scalar.copy, g_w2[:], w2[:])
+        quantise(cw[:, 2, :], sw[:, 2, :], g_wc[:])
         nc.vector.tensor_copy(out=b1f[:], in_=b1raw[:])
-        nc.vector.tensor_scalar(out=b1s[:], in0=b1raw[:], scalar1=SLOPE, scalar2=None, op0=ALU.mult)
-        layer1(0, False)
-        sine_stream(5)
+        quantise_sin(0)
+        layer1(0, 0, 2)
+        sine_stream(3)
+        group_sines(1, nc.scalar.copy)
         quantise(cw[:, 3, :], sw[:, 3, :], g_w2[:])
-        quantise_sin(1)
-        layer1(1, True)
-        hidden_leaky_planes(0)
+        sine_stream(2)
+        hidden_leaky(0, 0)
+        hidden_leaky(0, 1)
         quantise_hidden(0, 0)
+        layer2(0, 0)
         quantise_hidden(0, 1)
-        outputs(0, (), (lambda: quantise_sin(2), lambda: layer1(2, True)))
+        layer2(0, 1)
+        sine_stream(1)
+        add_bias(0, 0)
+        add_bias(0, 1)
+        finish(0, 0)
+        quantise_sin(1)
+        layer1(1, 0, 2)
+        sine_stream(2)
+        group_sines(2, nc.scalar.copy)
+        finish(0, 1)
+        add_bias(0, 2)
+        add_bias(0, 3)
+        finish(0, 2)
         hidden_leaky(1, 0)
+        finish(0, 3)
         hidden_leaky(1, 1)
         quantise_hidden(1, 0)
+        layer2(1, 0)
         quantise_hidden(1, 1)
-        outputs(1, (lambda: hidden_leaky(2, 0),), (lambda: hidden_leaky(2, 1),))
+        layer2(1, 1)
+        quantise_sin(2)
+        layer1(2, 0)
+        layer1(2, 1)
+        add_bias(1, 0)
+        add_bias(1, 1)
+        finish(1, 0)
+        add_bias(1, 2)
+        finish(1, 1)
+        add_bias(1, 3)
+        finish(1, 2)
+        hidden_leaky(2, 0)
+        finish(1, 3)
         quantise_hidden(2, 0)
+        layer2(2, 0)
+        hidden_leaky(2, 1)
+        add_bias(2, 0)
         quantise_hidden(2, 1)
-        outputs(2, (), ())
+        layer2(2, 1)
+        add_bias(2, 1)
+        finish(2, 0)
+        finish(2, 1)
+        add_bias(2, 2)
+        add_bias(2, 3)
+        finish(2, 2)
+        finish(2, 3)

@@ -2,7 +2,6 @@ import math
 from contextlib import ExitStack
 
 import concourse.mybir as mybir
-from concourse.masks import make_identity
 
 F32 = mybir.dt.float32
 BF16 = mybir.dt.bfloat16
@@ -81,8 +80,6 @@ def tile_claimencoder_kernel(
 
         lane = keep.tile([P, 1], I32)
         nc.gpsimd.iota(lane[:], pattern=[[0, 1]], base=0, channel_multiplier=1)
-        w1s = keep.tile([P, SLOTS, H], BF16)
-        nc.gpsimd.dma_start(out=w1s[:], in_=W1[0:640, :].rearrange("(p s) n -> p s n", s=SLOTS))
 
         warm = keep.tile([P, 1], F32)
         nc.vector.memset(warm[:], 0.0)
@@ -99,14 +96,15 @@ def tile_claimencoder_kernel(
         nc.gpsimd.dma_start(out=num_wb[4:5, 2, :], in_=row(wd_b))
         for t, scal in enumerate((time_s, wait_src, wait_dst)):
             load(rows_num[1 + t : 2 + t, :], row(scal))
-
-        xy = keep.tile([P, 2 * B], BF16)
+        rows_xy = keep.tile([P, 2 * B], BF16)
+        fill(rows_xy[:], TWO_ONES)
         flat_s = src_xy.rearrange("b c -> (b c)")
         flat_d = dst_xy.rearrange("b c -> (b c)")
         for g, points in enumerate((flat_s, flat_s[1 : 2 * B], flat_d, flat_d[1 : 2 * B])):
             n = points.shape[0]
-            load(xy[32 * g : 32 * g + 32, 0:n], points.partition_broadcast(32))
-        xs = xy[:].rearrange("p (b c) -> p b c", c=2)[:, :, 0]
+            load(rows_xy[32 * g : 32 * g + 1, 0:n], row(points))
+        w1s = keep.tile([P, SLOTS, H], BF16)
+        load(w1s[:], W1[0:640, :].rearrange("(p s) n -> p s n", s=SLOTS))
 
         pw = keep.tile([P, SLOTS], BF16)
         pb = keep.tile([P, SLOTS], BF16)
@@ -117,14 +115,17 @@ def tile_claimencoder_kernel(
             (dst_wsy, dst_bsy, dst_wcy, dst_bcy),
         )
         for g, vecs in enumerate(groups):
-            queue = nc.gpsimd if g == 3 else nc.sync
             for i, vec in enumerate(vecs):
                 dst = pb if i % 2 else pw
                 lo = 32 * g + 16 * (i // 2)
-                queue.dma_start(out=dst[lo : lo + 16, :], in_=vec.rearrange("(l s) -> l s", s=SLOTS))
+                nc.sync.dma_start(out=dst[lo : lo + 16, :], in_=vec.rearrange("(l s) -> l s", s=SLOTS))
 
+        sel = keep.tile([P, P], BF16)
+        fill(sel[:], 0)
         g_c = keep.tile([P, CH, 4], BF16, align_bytes=64)
         fill(flat(g_c), 0)
+        for g in range(4):
+            fill(sel[32 * g : 32 * g + 1, 32 * g : 32 * g + 32], TWO_ONES)
         bit = keep.tile([P, 1], I32)
         nc.vector.tensor_scalar(out=bit[:], in0=lane[:], scalar1=16, scalar2=None, op0=ALU.bitwise_and)
         g_wb = keep.tile([P, H, 4], BF16, align_bytes=64)
@@ -143,13 +144,14 @@ def tile_claimencoder_kernel(
         b1raw = keep.tile([P, 4], BF16)
         with nc.allow_non_contiguous_dma(reason="512 bias values, one per partition and output tile"):
             nc.gpsimd.dma_start(out=b1raw[:], in_=b1.rearrange("(m p) -> p m", p=P))
-        b2bc = keep.tile([P, H], BF16)
-        nc.gpsimd.dma_start(out=b2bc[:], in_=b2.partition_broadcast(P))
+        b2rows = keep.tile([P, H], BF16)
+        nc.gpsimd.memset(b2rows[:].bitcast(I32), TWO_ONES)
+        nc.gpsimd.dma_start(out=b2rows[0:128:32, :], in_=b2.partition_broadcast(4))
+        b2bc = keep.tile([P, H], F32)
         g_b1 = keep.tile([P, CH, 4], BF16, align_bytes=64)
         clear_late(g_b1)
         g_bs = (g_b0, g_b1, g_b0)
-        ident = keep.tile([P, P], F32)
-        make_identity(nc, ident[:])
+        xs = keep.tile([P, B], BF16)
 
         cw = keep.tile([P, 4, H], U32, align_bytes=64)
         sw = keep.tile([P, 4, H], U8, align_bytes=64)
@@ -159,8 +161,6 @@ def tile_claimencoder_kernel(
         sb = keep.tile([P, SLOTS], F32)
         bq = keep.tile([P, SLOTS], F32)
         b1f = keep.tile([P, 4], F32)
-        b2f = keep.tile([P, H], F32)
-        b2c = keep.tile([P, 4], F32)
         g_w1 = keep.tile([P, H, 4], BF16, align_bytes=64)
         g_w2 = keep.tile([P, H, 4], BF16, align_bytes=64)
 
@@ -175,6 +175,18 @@ def tile_claimencoder_kernel(
                 out=bq[:], in0=pb[:], scalar1=phase[:, 0:1], scalar2=1.0 / TWO_PI, op0=ALU.add, op1=ALU.mult
             )
             nc.vector.tensor_scalar(out=sb[:], in0=pb[:], scalar1=phase[:, 0:1], scalar2=None, op0=ALU.add)
+
+        def spread_points():
+            pairs = rows_xy[:].rearrange("p (b c) -> p b c", c=2)
+            for c in range(NCH):
+                xps = psum.tile([P, CH], BF16, tag="bank")
+                nc.tensor.matmul(out=xps[:], lhsT=sel[:], rhs=pairs[:, chunk(c), 0], start=True, stop=True)
+                nc.scalar.copy(out=xs[:, chunk(c)], in_=xps[:])
+
+        def spread_bias():
+            bps = psum.tile([P, H], F32, tag="bank")
+            nc.tensor.matmul(out=bps[:], lhsT=sel[:], rhs=b2rows[:], start=True, stop=True)
+            nc.scalar.copy(out=b2bc[:], in_=bps[:])
 
         banks = {}
         smalls = {}
@@ -324,65 +336,16 @@ def tile_claimencoder_kernel(
             )
             store(c, j, res)
 
-        def bias_columns():
-            nc.scalar.copy(out=b2f[:], in_=b2bc[:])
-            bps = psum.tile([P, 4, P], F32, tag="bank")
-            for m in range(4):
-                nc.tensor.transpose(out=bps[:, m, :], in_=b2f[:, m * P : (m + 1) * P], identity=ident[:])
-            nc.scalar.copy(out=b2c[:], in_=bps[:, :, 0])
-
-        upright = {}
-        turned = {}
-        turned_lows = {}
-
-        def turned_layer2(c, half):
-            ch, sh = hidden[(c, half)]
-            vt = work.tile([P, 4, HALF], F32, tag="vt")
-            upright[(c, half)] = vt
-            for pair in range(2):
-                acc = psum.tile([P, 2, HALF], F32, tag="bank")
-                for i in range(2):
-                    m = 2 * pair + i
-                    ms = slice(m * P, (m + 1) * P)
-                    nc.tensor.matmul_mx(
-                        out=acc[:, i, :],
-                        lhsT=cw[:, 3, ms].bitcast(FP8X4), lhsT_scale=sw[:, 3, ms],
-                        rhs=ch[:].bitcast(FP8X4), rhs_scale=sh[:],
-                        start=True, stop=True,
-                    )
-                for i in range(2):
-                    m = 2 * pair + i
-                    nc.scalar.activation(
-                        out=vt[:, m, :], in_=acc[:, i, :], func=ACT.Identity, bias=b2c[:, m : m + 1], scale=1.0
-                    )
-
-        def turn_back(c, half):
-            for i in range(2):
-                j = 2 * half + i
-                tps = psum.tile([P, H], F32, tag="bank")
-                for m in range(4):
-                    nc.tensor.transpose(
-                        out=tps[:, m * P : (m + 1) * P],
-                        in_=upright[(c, half)][:, m, i * P : (i + 1) * P], identity=ident[:],
-                    )
-                turned[(c, j)] = tps
-                tlow = work.tile([P, H], F32, tag="tlow", bufs=4)
-                nc.scalar.activation(out=tlow[:], in_=tps[:], func=ACT.Copy, scale=SLOPE)
-                turned_lows[(c, j)] = tlow
-
-        def finish_turned(c, j):
-            res = work.tile([P, H], F32, tag="res", bufs=4)
-            nc.vector.tensor_tensor(out=res[:], in0=turned[(c, j)][:], in1=turned_lows[(c, j)][:], op=ALU.max)
-            store(c, j, res)
 
         num_products(0)
+        spread_points()
         num_products(1)
-        regroup(nc.vector.tensor_copy, g_w1[:], w1s[:, 0:4, :])
         num_leaky(0)
+        regroup(nc.vector.tensor_copy, g_w1[:], w1s[:, 0:4, :])
+        quantise_num(0)
         quantise(cw[:, 0, :], sw[:, 0, :], g_w1[:])
         num_products(2)
         nc.scalar.copy(out=g_wb[:, :, 0], in_=w1s[:, 4, :])
-        quantise_num(0)
         num_leaky(1)
         constants()
         sine_stream(3)
@@ -397,6 +360,7 @@ def tile_claimencoder_kernel(
         regroup(nc.scalar.copy, g_w2[:], w2[:])
         quantise(cw[:, 2, :], sw[:, 2, :], g_wc[:])
         nc.vector.tensor_copy(out=b1f[:], in_=b1raw[:])
+        spread_bias()
         quantise_sin(0)
         layer1(0, 0, 2)
         sine_stream(3)

@@ -75,8 +75,6 @@ def tile_claimencoder_kernel(
         def flat(grouped):
             return grouped[:].rearrange("p n t -> p (n t)")
 
-        def clear_late(grouped):
-            nc.gpsimd.memset(flat(grouped).bitcast(I32), 0)
 
         lane = keep.tile([P, 1], I32)
         nc.gpsimd.iota(lane[:], pattern=[[0, 1]], base=0, channel_multiplier=1)
@@ -135,22 +133,20 @@ def tile_claimencoder_kernel(
         g_wc = keep.tile([P, H, 4], BF16, align_bytes=64)
         fill(flat(g_wc), 0)
 
-        w1n = keep.tile([P, 3, H], BF16)
-        nc.gpsimd.dma_start(out=w1n[:], in_=W1[640:1024, :].rearrange("(t p) n -> p t n", p=P))
-        w2 = keep.tile([P, 4, H], BF16)
-        nc.gpsimd.dma_start(out=w2[:], in_=W2.rearrange("(t p) n -> p t n", p=P))
         g_b0 = keep.tile([P, CH, 4], BF16, align_bytes=64)
-        clear_late(g_b0)
-        b1raw = keep.tile([P, 4], BF16)
-        with nc.allow_non_contiguous_dma(reason="512 bias values, one per partition and output tile"):
-            nc.gpsimd.dma_start(out=b1raw[:], in_=b1.rearrange("(m p) -> p m", p=P))
-        b2rows = keep.tile([P, H], BF16)
-        nc.gpsimd.memset(b2rows[:].bitcast(I32), TWO_ONES)
-        nc.gpsimd.dma_start(out=b2rows[0:128:32, :], in_=b2.partition_broadcast(4))
-        b2bc = keep.tile([P, H], F32)
+        fill(flat(g_b0), 0)
         g_b1 = keep.tile([P, CH, 4], BF16, align_bytes=64)
-        clear_late(g_b1)
+        fill(flat(g_b1), 0)
         g_bs = (g_b0, g_b1, g_b0)
+        rows_b = keep.tile([P, 2, H], BF16)
+        fill(rows_b[:].rearrange("p v n -> p (v n)"), TWO_ONES)
+        load(rows_b[0:1, 0, :], row(b1))
+        load(rows_b[0:128:32, 1, :], b2.partition_broadcast(4))
+        w1n = keep.tile([P, 3, H], BF16)
+        load(w1n[:], W1[640:1024, :].rearrange("(t p) n -> p t n", p=P))
+        w2 = keep.tile([P, 4, H], BF16)
+        load(w2[:], W2.rearrange("(t p) n -> p t n", p=P))
+        b2bc = keep.tile([P, H], F32)
         xs = keep.tile([P, B], BF16)
 
         cw = keep.tile([P, 4, H], U32, align_bytes=64)
@@ -183,10 +179,16 @@ def tile_claimencoder_kernel(
                 nc.tensor.matmul(out=xps[:], lhsT=sel[:], rhs=pairs[:, chunk(c), 0], start=True, stop=True)
                 nc.scalar.copy(out=xs[:, chunk(c)], in_=xps[:])
 
-        def spread_bias():
+        def spread_biases():
             bps = psum.tile([P, H], F32, tag="bank")
-            nc.tensor.matmul(out=bps[:], lhsT=sel[:], rhs=b2rows[:], start=True, stop=True)
+            nc.tensor.matmul(out=bps[:], lhsT=sel[:], rhs=rows_b[:, 1, :], start=True, stop=True)
             nc.scalar.copy(out=b2bc[:], in_=bps[:])
+            cps = psum.tile([P, 4], F32, tag="bank")
+            for m in range(4):
+                nc.tensor.matmul(
+                    out=cps[:, m : m + 1], lhsT=rows_b[:, 0, m * P : (m + 1) * P], rhs=sel[:, 0:1], start=True, stop=True
+                )
+            nc.scalar.copy(out=b1f[:], in_=cps[:])
 
         banks = {}
         smalls = {}
@@ -359,8 +361,7 @@ def tile_claimencoder_kernel(
         quantise_num(2)
         regroup(nc.scalar.copy, g_w2[:], w2[:])
         quantise(cw[:, 2, :], sw[:, 2, :], g_wc[:])
-        nc.vector.tensor_copy(out=b1f[:], in_=b1raw[:])
-        spread_bias()
+        spread_biases()
         quantise_sin(0)
         layer1(0, 0, 2)
         sine_stream(3)

@@ -79,10 +79,14 @@ def tile_claimencoder_kernel(
         lane = keep.tile([P, 1], I32)
         nc.gpsimd.iota(lane[:], pattern=[[0, 1]], base=0, channel_multiplier=1)
 
+        w1s = keep.tile([P, SLOTS, H], BF16)
+        load(w1s[:], W1[0:640, :].rearrange("(p s) n -> p s n", s=SLOTS))
         warm = keep.tile([P, 1], F32)
         nc.vector.memset(warm[:], 0.0)
         warmed = keep.tile([P, 1], F32)
         nc.scalar.activation(out=warmed[:], in_=warm[:], func=ACT.Sin)
+        idle = keep.tile([P, 4 * P], BF16, align_bytes=64)
+        fill(idle[:], 0)
         num_wb = keep.tile([P, 3, P], BF16)
         fill(num_wb[:].rearrange("p t n -> p (t n)"), 0)
         rows_num = keep.tile([P, B], BF16)
@@ -90,10 +94,13 @@ def tile_claimencoder_kernel(
         for t, w_t in enumerate((t_w, ws_w, wd_w)):
             load(num_wb[1 + t : 2 + t, t, :], row(w_t))
         load(num_wb[4:5, 0, :], row(t_b))
-        load(num_wb[4:5, 1, :], row(ws_b))
+        nc.gpsimd.dma_start(out=num_wb[4:5, 1, :], in_=row(ws_b))
         nc.gpsimd.dma_start(out=num_wb[4:5, 2, :], in_=row(wd_b))
         for t, scal in enumerate((time_s, wait_src, wait_dst)):
             load(rows_num[1 + t : 2 + t, :], row(scal))
+        idle_codes = keep.tile([P, P], U32, align_bytes=64)
+        idle_scales = keep.tile([P, P], U8, align_bytes=64)
+        nc.vector.quantize_mx(out=idle_codes[:].bitcast(FP8X4), scales=idle_scales[:], in_=idle[:])
         rows_xy = keep.tile([P, 2 * B], BF16)
         fill(rows_xy[:], TWO_ONES)
         flat_s = src_xy.rearrange("b c -> (b c)")
@@ -101,9 +108,6 @@ def tile_claimencoder_kernel(
         for g, points in enumerate((flat_s, flat_s[1 : 2 * B], flat_d, flat_d[1 : 2 * B])):
             n = points.shape[0]
             load(rows_xy[32 * g : 32 * g + 1, 0:n], row(points))
-        w1s = keep.tile([P, SLOTS, H], BF16)
-        load(w1s[:], W1[0:640, :].rearrange("(p s) n -> p s n", s=SLOTS))
-
         pw = keep.tile([P, SLOTS], BF16)
         pb = keep.tile([P, SLOTS], BF16)
         groups = (
@@ -134,14 +138,10 @@ def tile_claimencoder_kernel(
         fill(flat(g_wc), 0)
 
         g_b0 = keep.tile([P, CH, 4], BF16, align_bytes=64)
-        fill(flat(g_b0), 0)
+        nc.scalar.copy(out=flat(g_b0), in_=flat(g_c))
         g_b1 = keep.tile([P, CH, 4], BF16, align_bytes=64)
-        fill(flat(g_b1), 0)
+        nc.scalar.copy(out=flat(g_b1), in_=flat(g_c))
         g_bs = (g_b0, g_b1, g_b0)
-        rows_b = keep.tile([P, 2, H], BF16)
-        fill(rows_b[:].rearrange("p v n -> p (v n)"), TWO_ONES)
-        load(rows_b[0:1, 0, :], row(b1))
-        load(rows_b[0:128:32, 1, :], b2.partition_broadcast(4))
         w1n = keep.tile([P, 3, H], BF16)
         load(w1n[:], W1[640:1024, :].rearrange("(t p) n -> p t n", p=P))
         w2 = keep.tile([P, 4, H], BF16)
@@ -179,14 +179,28 @@ def tile_claimencoder_kernel(
                 nc.tensor.matmul(out=xps[:], lhsT=sel[:], rhs=pairs[:, chunk(c), 0], start=True, stop=True)
                 nc.scalar.copy(out=xs[:, chunk(c)], in_=xps[:])
 
+        def warm_up(passes):
+            scratch = psum.tile([P, P], F32, tag="bank")
+            for i in range(passes):
+                nc.tensor.matmul_mx(
+                    out=scratch[:],
+                    lhsT=idle_codes[:].bitcast(FP8X4), lhsT_scale=idle_scales[:],
+                    rhs=idle_codes[:].bitcast(FP8X4), rhs_scale=idle_scales[:],
+                    start=True, stop=True,
+                )
+
+        def load_biases():
+            load(rows_num[0:1, H : 2 * H], row(b1))
+            load(rows_num[0:128:32, 0:H], b2.partition_broadcast(4))
+
         def spread_biases():
             bps = psum.tile([P, H], F32, tag="bank")
-            nc.tensor.matmul(out=bps[:], lhsT=sel[:], rhs=rows_b[:, 1, :], start=True, stop=True)
+            nc.tensor.matmul(out=bps[:], lhsT=sel[:], rhs=rows_num[:, 0:H], start=True, stop=True)
             nc.scalar.copy(out=b2bc[:], in_=bps[:])
             cps = psum.tile([P, 4], F32, tag="bank")
             for m in range(4):
                 nc.tensor.matmul(
-                    out=cps[:, m : m + 1], lhsT=rows_b[:, 0, m * P : (m + 1) * P], rhs=sel[:, 0:1], start=True, stop=True
+                    out=cps[:, m : m + 1], lhsT=rows_num[:, H + m * P : H + (m + 1) * P], rhs=sel[:, 0:1], start=True, stop=True
                 )
             nc.scalar.copy(out=b1f[:], in_=cps[:])
 
@@ -339,14 +353,16 @@ def tile_claimencoder_kernel(
             store(c, j, res)
 
 
+        warm_up(16)
+        regroup(nc.vector.tensor_copy, g_w1[:], w1s[:, 0:4, :])
         num_products(0)
         spread_points()
         num_products(1)
         num_leaky(0)
-        regroup(nc.vector.tensor_copy, g_w1[:], w1s[:, 0:4, :])
-        quantise_num(0)
         quantise(cw[:, 0, :], sw[:, 0, :], g_w1[:])
+        quantise_num(0)
         num_products(2)
+        load_biases()
         nc.scalar.copy(out=g_wb[:, :, 0], in_=w1s[:, 4, :])
         num_leaky(1)
         constants()

@@ -2,6 +2,7 @@ import math
 from contextlib import ExitStack
 
 import concourse.mybir as mybir
+from concourse.masks import make_identity
 
 F32 = mybir.dt.float32
 BF16 = mybir.dt.bfloat16
@@ -120,7 +121,8 @@ def tile_claimencoder_kernel(
             for i, vec in enumerate(vecs):
                 dst = pb if i % 2 else pw
                 lo = 32 * g + 16 * (i // 2)
-                nc.sync.dma_start(out=dst[lo : lo + 16, :], in_=vec.rearrange("(l s) -> l s", s=SLOTS))
+                queue = nc.gpsimd if 4 * g + i >= 10 else nc.sync
+                queue.dma_start(out=dst[lo : lo + 16, :], in_=vec.rearrange("(l s) -> l s", s=SLOTS))
 
         sel = keep.tile([P, P], BF16)
         fill(sel[:], 0)
@@ -148,6 +150,9 @@ def tile_claimencoder_kernel(
         load(w2[:], W2.rearrange("(t p) n -> p t n", p=P))
         b2bc = keep.tile([P, H], F32)
         xs = keep.tile([P, B], BF16)
+        ident = keep.tile([P, P], F32)
+        make_identity(nc, ident[:])
+        b2c = keep.tile([P, 4], F32)
 
         cw = keep.tile([P, 4, H], U32, align_bytes=64)
         sw = keep.tile([P, 4, H], U8, align_bytes=64)
@@ -246,7 +251,7 @@ def tile_claimencoder_kernel(
             turn_tiles[(c, s)] = turn
 
         def fracs(c, s):
-            frac = work.tile([P, CH], F32, tag="frac", bufs=8)
+            frac = work.tile([P, CH], F32, tag="frac", bufs=12)
             nc.vector.scalar_tensor_tensor(
                 out=frac[:], in0=xs[:, chunk(c)], scalar=wq[:, s : s + 1], in1=turn_tiles[(c, s)][:],
                 op0=ALU.mult, op1=ALU.subtract,
@@ -280,29 +285,55 @@ def tile_claimencoder_kernel(
             regroup(copy, g_a[:], plane_tiles[c][:])
             grouped_a[c] = g_a
 
-        def quantise_sin(c):
-            quantise(cf[:, 1, chunk(c)], sf[:, 1, chunk(c)], g_bs[c][:])
-            quantise(cf[:, 0, chunk(c)], sf[:, 0, chunk(c)], grouped_a[c][:])
-
         biased = {}
 
-        def layer1(c, half, width=1):
-            pre1 = work.tile([P, 4, width * HALF], F32, tag="pre1", bufs=3)
+        open_sums = {}
+
+        def layer1_pass(c, i, m, cols, acc, start, stop):
+            ms = slice(m * P, (m + 1) * P)
+            nc.tensor.matmul_mx(
+                out=acc[:],
+                lhsT=cw[:, i, ms].bitcast(FP8X4), lhsT_scale=sw[:, i, ms],
+                rhs=cf[:, i, cols].bitcast(FP8X4), rhs_scale=sf[:, i, cols],
+                start=start, stop=stop,
+            )
+
+        def columns(c, half, width):
             lo = c * CH + half * HALF
-            cols = slice(lo, lo + width * HALF)
+            return slice(lo, lo + width * HALF)
+
+        def layer1_open(c, half, width):
+            cols = columns(c, half, width)
             for m in range(4):
-                ms = slice(m * P, (m + 1) * P)
                 acc = psum.tile([P, width * HALF], F32, tag="bank")
-                for n, i in enumerate((2, 1, 0)):
-                    nc.tensor.matmul_mx(
-                        out=acc[:],
-                        lhsT=cw[:, i, ms].bitcast(FP8X4), lhsT_scale=sw[:, i, ms],
-                        rhs=cf[:, i, cols].bitcast(FP8X4), rhs_scale=sf[:, i, cols],
-                        start=(n == 0), stop=(n == 2),
-                    )
+                layer1_pass(c, 2, m, cols, acc, True, False)
+                open_sums[(c, half, m)] = acc
+
+        def layer1_more(c, half, width):
+            cols = columns(c, half, width)
+            for m in range(4):
+                layer1_pass(c, 1, m, cols, open_sums[(c, half, m)], False, False)
+
+        def layer1_close(c, half, width):
+            cols = columns(c, half, width)
+            pre1 = work.tile([P, 4, width * HALF], F32, tag="pre1", bufs=3)
+            for m in range(4):
+                acc = open_sums[(c, half, m)]
+                layer1_pass(c, 0, m, cols, acc, False, True)
                 nc.scalar.activation(out=pre1[:, m, :], in_=acc[:], func=ACT.Identity, bias=b1f[:, m : m + 1], scale=1.0)
             for w in range(width):
                 biased[(c, half + w)] = pre1[:, :, w * HALF : (w + 1) * HALF]
+
+        def quantise_and_layer1(c, width):
+            layer1_open(c, 0, width)
+            quantise(cf[:, 1, chunk(c)], sf[:, 1, chunk(c)], g_bs[c][:])
+            layer1_more(c, 0, width)
+            quantise(cf[:, 0, chunk(c)], sf[:, 0, chunk(c)], grouped_a[c][:])
+            layer1_close(c, 0, width)
+            if width == 1:
+                layer1_open(c, 1, 1)
+                layer1_more(c, 1, 1)
+                layer1_close(c, 1, 1)
 
         grouped_h = {}
         hidden = {}
@@ -336,7 +367,7 @@ def tile_claimencoder_kernel(
                 sums[(c, 2 * half + i)] = acc
 
         def add_bias(c, j):
-            pre = work.tile([P, H], F32, tag="pre", bufs=4)
+            pre = work.tile([P, H], F32, tag="pre", bufs=6)
             nc.vector.tensor_tensor(out=pre[:], in0=sums[(c, j)][:], in1=b2bc[:], op=ALU.add)
             pres[(c, j)] = pre
 
@@ -345,13 +376,62 @@ def tile_claimencoder_kernel(
             nc.sync.dma_start(out=out[lo : lo + P, :], in_=res[:])
 
         def finish(c, j):
-            res = work.tile([P, H], F32, tag="res", bufs=4)
+            res = work.tile([P, H], F32, tag="res", bufs=12)
             pre = pres[(c, j)]
             nc.vector.scalar_tensor_tensor(
                 out=res[:], in0=pre[:], scalar=SLOPE, in1=pre[:], op0=ALU.mult, op1=ALU.max
             )
             store(c, j, res)
 
+        def bias_columns():
+            bps = psum.tile([P, 4, P], F32, tag="bank")
+            for m in range(4):
+                nc.tensor.transpose(out=bps[:, m, :], in_=b2bc[:, m * P : (m + 1) * P], identity=ident[:])
+            nc.scalar.copy(out=b2c[:], in_=bps[:, :, 0])
+
+        upright = {}
+        turned = {}
+        turned_lows = {}
+
+        def turned_layer2(c, half):
+            ch, sh = hidden[(c, half)]
+            vt = work.tile([P, 4, HALF], F32, tag="vt")
+            upright[(c, half)] = vt
+            for pair in range(2):
+                acc = psum.tile([P, 2, HALF], F32, tag="bank")
+                for i in range(2):
+                    m = 2 * pair + i
+                    ms = slice(m * P, (m + 1) * P)
+                    nc.tensor.matmul_mx(
+                        out=acc[:, i, :],
+                        lhsT=cw[:, 3, ms].bitcast(FP8X4), lhsT_scale=sw[:, 3, ms],
+                        rhs=ch[:].bitcast(FP8X4), rhs_scale=sh[:],
+                        start=True, stop=True,
+                    )
+                for i in range(2):
+                    m = 2 * pair + i
+                    nc.scalar.activation(
+                        out=vt[:, m, :], in_=acc[:, i, :], func=ACT.Identity, bias=b2c[:, m : m + 1], scale=1.0
+                    )
+
+        def turn_back(c, half):
+            for i in range(2):
+                j = 2 * half + i
+                tps = psum.tile([P, H], F32, tag="bank")
+                for m in range(4):
+                    nc.tensor.transpose(
+                        out=tps[:, m * P : (m + 1) * P],
+                        in_=upright[(c, half)][:, m, i * P : (i + 1) * P], identity=ident[:],
+                    )
+                turned[(c, j)] = tps
+                tlow = work.tile([P, H], F32, tag="tlow", bufs=4)
+                nc.scalar.activation(out=tlow[:], in_=tps[:], func=ACT.Copy, scale=SLOPE)
+                turned_lows[(c, j)] = tlow
+
+        def finish_turned(c, j):
+            res = work.tile([P, H], F32, tag="res", bufs=12)
+            nc.vector.tensor_tensor(out=res[:], in0=turned[(c, j)][:], in1=turned_lows[(c, j)][:], op=ALU.max)
+            store(c, j, res)
 
         warm_up(16)
         regroup(nc.vector.tensor_copy, g_w1[:], w1s[:, 0:4, :])
@@ -378,59 +458,51 @@ def tile_claimencoder_kernel(
         regroup(nc.scalar.copy, g_w2[:], w2[:])
         quantise(cw[:, 2, :], sw[:, 2, :], g_wc[:])
         spread_biases()
-        quantise_sin(0)
-        layer1(0, 0, 2)
+        quantise_and_layer1(0, 2)
         sine_stream(3)
         group_sines(1, nc.scalar.copy)
+        bias_columns()
         quantise(cw[:, 3, :], sw[:, 3, :], g_w2[:])
-        sine_stream(2)
+        sine_stream(5)
+        group_sines(2, nc.scalar.copy)
         hidden_leaky(0, 0)
         hidden_leaky(0, 1)
         quantise_hidden(0, 0)
         layer2(0, 0)
         quantise_hidden(0, 1)
         layer2(0, 1)
-        sine_stream(1)
+        quantise_and_layer1(1, 2)
         add_bias(0, 0)
         add_bias(0, 1)
         finish(0, 0)
-        quantise_sin(1)
-        layer1(1, 0, 2)
-        sine_stream(2)
-        group_sines(2, nc.scalar.copy)
-        finish(0, 1)
         add_bias(0, 2)
+        finish(0, 1)
         add_bias(0, 3)
+        quantise_and_layer1(2, 1)
         finish(0, 2)
-        hidden_leaky(1, 0)
         finish(0, 3)
+        hidden_leaky(1, 0)
         hidden_leaky(1, 1)
         quantise_hidden(1, 0)
-        layer2(1, 0)
+        turned_layer2(1, 0)
         quantise_hidden(1, 1)
-        layer2(1, 1)
-        quantise_sin(2)
-        layer1(2, 0)
-        layer1(2, 1)
-        add_bias(1, 0)
-        add_bias(1, 1)
-        finish(1, 0)
-        add_bias(1, 2)
-        finish(1, 1)
-        add_bias(1, 3)
-        finish(1, 2)
+        turned_layer2(1, 1)
         hidden_leaky(2, 0)
-        finish(1, 3)
+        turn_back(1, 0)
+        hidden_leaky(2, 1)
+        turn_back(1, 1)
         quantise_hidden(2, 0)
         layer2(2, 0)
-        hidden_leaky(2, 1)
-        add_bias(2, 0)
         quantise_hidden(2, 1)
-        layer2(2, 1)
+        turned_layer2(2, 1)
+        finish_turned(1, 0)
+        finish_turned(1, 1)
+        add_bias(2, 0)
         add_bias(2, 1)
+        finish_turned(1, 2)
+        finish_turned(1, 3)
+        turn_back(2, 1)
         finish(2, 0)
         finish(2, 1)
-        add_bias(2, 2)
-        add_bias(2, 3)
-        finish(2, 2)
-        finish(2, 3)
+        finish_turned(2, 2)
+        finish_turned(2, 3)

import math
from contextlib import ExitStack

import concourse.mybir as mybir
from concourse.masks import make_identity

F32 = mybir.dt.float32
BF16 = mybir.dt.bfloat16
I32 = mybir.dt.int32
U32 = mybir.dt.uint32
U8 = mybir.dt.uint8
FP8X4 = mybir.dt.float8_e4m3fn_x4
ALU = mybir.AluOpType
ACT = mybir.ActivationFunctionType

P = 128
B = 1536
CH = 512
HALF = CH // 2
NCH = B // CH
H = 512
SLOTS = 5
TWO_PI = 2.0 * math.pi
SLOPE = 0.01
TWO_ONES = 0x3F803F80

FLOPS = 2 * B * 1024 * H + 2 * B * H * H


def row(vec):
    return vec.rearrange("(o n) -> o n", o=1)


def by_runs_out(grouped):
    return grouped.rearrange("p (c i) t -> p c t i", i=4)


def by_runs_in(planes):
    return planes.rearrange("p t (c i) -> p c t i", i=4)


def regroup(copy, dst, src):
    copy(out=by_runs_out(dst), in_=by_runs_in(src))


def chunk(c):
    return slice(c * CH, (c + 1) * CH)


def halves(half):
    return slice(half * HALF, (half + 1) * HALF)


def tile_claimencoder_kernel(
    tc,
    src_xy, dst_xy, time_s, wait_src, wait_dst,
    src_wsx, src_bsx, src_wcx, src_bcx, src_wsy, src_bsy, src_wcy, src_bcy,
    dst_wsx, dst_bsx, dst_wcx, dst_bcx, dst_wsy, dst_bsy, dst_wcy, dst_bcy,
    t_w, t_b, ws_w, ws_b, wd_w, wd_b,
    W1, b1, W2, b2,
    out,
):
    nc = tc.nc
    with ExitStack() as ctx:
        keep = ctx.enter_context(tc.tile_pool(name="keep", bufs=1))
        work = ctx.enter_context(tc.tile_pool(name="work", bufs=2))
        psum = ctx.enter_context(tc.psum_pool(name="psum", bufs=8))
        ctx.enter_context(tc.manual_schedule())

        def load(dst, src):
            nc.sync.dma_start(out=dst, in_=src)

        def fill(bf16_view, word):
            nc.vector.memset(bf16_view.bitcast(I32), word)

        def flat(grouped):
            return grouped[:].rearrange("p n t -> p (n t)")


        lane = keep.tile([P, 1], I32)
        nc.gpsimd.iota(lane[:], pattern=[[0, 1]], base=0, channel_multiplier=1)

        w1s = keep.tile([P, SLOTS, H], BF16)
        load(w1s[:], W1[0:640, :].rearrange("(p s) n -> p s n", s=SLOTS))
        warm = keep.tile([P, 1], F32)
        nc.vector.memset(warm[:], 0.0)
        warmed = keep.tile([P, 1], F32)
        nc.scalar.activation(out=warmed[:], in_=warm[:], func=ACT.Sin)
        idle = keep.tile([P, 4 * P], BF16, align_bytes=64)
        fill(idle[:], 0)
        num_wb = keep.tile([P, 3, P], BF16)
        fill(num_wb[:].rearrange("p t n -> p (t n)"), 0)
        rows_num = keep.tile([P, B], BF16)
        fill(rows_num[:], TWO_ONES)
        for t, w_t in enumerate((t_w, ws_w, wd_w)):
            load(num_wb[1 + t : 2 + t, t, :], row(w_t))
        load(num_wb[4:5, 0, :], row(t_b))
        nc.gpsimd.dma_start(out=num_wb[4:5, 1, :], in_=row(ws_b))
        nc.gpsimd.dma_start(out=num_wb[4:5, 2, :], in_=row(wd_b))
        for t, scal in enumerate((time_s, wait_src, wait_dst)):
            load(rows_num[1 + t : 2 + t, :], row(scal))
        idle_codes = keep.tile([P, P], U32, align_bytes=64)
        idle_scales = keep.tile([P, P], U8, align_bytes=64)
        nc.vector.quantize_mx(out=idle_codes[:].bitcast(FP8X4), scales=idle_scales[:], in_=idle[:])
        rows_xy = keep.tile([P, 2 * B], BF16)
        fill(rows_xy[:], TWO_ONES)
        flat_s = src_xy.rearrange("b c -> (b c)")
        flat_d = dst_xy.rearrange("b c -> (b c)")
        for g, points in enumerate((flat_s, flat_s[1 : 2 * B], flat_d, flat_d[1 : 2 * B])):
            n = points.shape[0]
            load(rows_xy[32 * g : 32 * g + 1, 0:n], row(points))
        pw = keep.tile([P, SLOTS], BF16)
        pb = keep.tile([P, SLOTS], BF16)
        groups = (
            (src_wsx, src_bsx, src_wcx, src_bcx),
            (src_wsy, src_bsy, src_wcy, src_bcy),
            (dst_wsx, dst_bsx, dst_wcx, dst_bcx),
            (dst_wsy, dst_bsy, dst_wcy, dst_bcy),
        )
        for g, vecs in enumerate(groups):
            for i, vec in enumerate(vecs):
                dst = pb if i % 2 else pw
                lo = 32 * g + 16 * (i // 2)
                queue = nc.gpsimd if 4 * g + i >= 10 else nc.sync
                queue.dma_start(out=dst[lo : lo + 16, :], in_=vec.rearrange("(l s) -> l s", s=SLOTS))

        sel = keep.tile([P, P], BF16)
        fill(sel[:], 0)
        g_c = keep.tile([P, CH, 4], BF16, align_bytes=64)
        fill(flat(g_c), 0)
        for g in range(4):
            fill(sel[32 * g : 32 * g + 1, 32 * g : 32 * g + 32], TWO_ONES)
        bit = keep.tile([P, 1], I32)
        nc.vector.tensor_scalar(out=bit[:], in0=lane[:], scalar1=16, scalar2=None, op0=ALU.bitwise_and)
        g_wb = keep.tile([P, H, 4], BF16, align_bytes=64)
        fill(flat(g_wb), 0)
        phase = keep.tile([P, 1], F32)
        nc.vector.tensor_scalar(out=phase[:], in0=bit[:], scalar1=math.pi / 32.0, scalar2=None, op0=ALU.mult)
        g_wc = keep.tile([P, H, 4], BF16, align_bytes=64)
        fill(flat(g_wc), 0)

        g_b0 = keep.tile([P, CH, 4], BF16, align_bytes=64)
        nc.scalar.copy(out=flat(g_b0), in_=flat(g_c))
        g_b1 = keep.tile([P, CH, 4], BF16, align_bytes=64)
        nc.scalar.copy(out=flat(g_b1), in_=flat(g_c))
        g_bs = (g_b0, g_b1, g_b0)
        w1n = keep.tile([P, 3, H], BF16)
        load(w1n[:], W1[640:1024, :].rearrange("(t p) n -> p t n", p=P))
        w2 = keep.tile([P, 4, H], BF16)
        load(w2[:], W2.rearrange("(t p) n -> p t n", p=P))
        b2bc = keep.tile([P, H], F32)
        xs = keep.tile([P, B], BF16)
        ident = keep.tile([P, P], F32)
        make_identity(nc, ident[:])
        b2c = keep.tile([P, 4], F32)

        cw = keep.tile([P, 4, H], U32, align_bytes=64)
        sw = keep.tile([P, 4, H], U8, align_bytes=64)
        cf = keep.tile([P, 3, B], U32, align_bytes=64)
        sf = keep.tile([P, 3, B], U8, align_bytes=64)
        wq = keep.tile([P, SLOTS], F32)
        sb = keep.tile([P, SLOTS], F32)
        bq = keep.tile([P, SLOTS], F32)
        b1f = keep.tile([P, 4], F32)
        g_w1 = keep.tile([P, H, 4], BF16, align_bytes=64)
        g_w2 = keep.tile([P, H, 4], BF16, align_bytes=64)

        def quantise(codes, scales, grouped):
            nc.vector.quantize_mx(
                out=codes.bitcast(FP8X4), scales=scales, in_=grouped.rearrange("p n t -> p (n t)")
            )

        def constants():
            nc.vector.tensor_scalar(out=wq[:], in0=pw[:], scalar1=1.0 / TWO_PI, scalar2=None, op0=ALU.mult)
            nc.vector.tensor_scalar(
                out=bq[:], in0=pb[:], scalar1=phase[:, 0:1], scalar2=1.0 / TWO_PI, op0=ALU.add, op1=ALU.mult
            )
            nc.vector.tensor_scalar(out=sb[:], in0=pb[:], scalar1=phase[:, 0:1], scalar2=None, op0=ALU.add)

        def spread_points():
            pairs = rows_xy[:].rearrange("p (b c) -> p b c", c=2)
            for c in range(NCH):
                xps = psum.tile([P, CH], BF16, tag="bank")
                nc.tensor.matmul(out=xps[:], lhsT=sel[:], rhs=pairs[:, chunk(c), 0], start=True, stop=True)
                nc.scalar.copy(out=xs[:, chunk(c)], in_=xps[:])

        def warm_up(passes):
            scratch = psum.tile([P, P], F32, tag="bank")
            for i in range(passes):
                nc.tensor.matmul_mx(
                    out=scratch[:],
                    lhsT=idle_codes[:].bitcast(FP8X4), lhsT_scale=idle_scales[:],
                    rhs=idle_codes[:].bitcast(FP8X4), rhs_scale=idle_scales[:],
                    start=True, stop=True,
                )

        def load_biases():
            load(rows_num[0:1, H : 2 * H], row(b1))
            load(rows_num[0:128:32, 0:H], b2.partition_broadcast(4))

        def spread_biases():
            bps = psum.tile([P, H], F32, tag="bank")
            nc.tensor.matmul(out=bps[:], lhsT=sel[:], rhs=rows_num[:, 0:H], start=True, stop=True)
            nc.scalar.copy(out=b2bc[:], in_=bps[:])
            cps = psum.tile([P, 4], F32, tag="bank")
            for m in range(4):
                nc.tensor.matmul(
                    out=cps[:, m : m + 1], lhsT=rows_num[:, H + m * P : H + (m + 1) * P], rhs=sel[:, 0:1], start=True, stop=True
                )
            nc.scalar.copy(out=b1f[:], in_=cps[:])

        banks = {}
        smalls = {}

        def num_products(c):
            for j in range(CH // P):
                vps = psum.tile([P, 4, P], F32, tag="bank")
                lo = c * CH + j * P
                for t in range(3):
                    nc.tensor.matmul(
                        out=vps[:, t, :], lhsT=num_wb[:, t, :], rhs=rows_num[:, lo : lo + P], start=True, stop=True
                    )
                small = work.tile([P, 3, P], F32, tag="small", bufs=8)
                nc.scalar.activation(out=small[:], in_=vps[:, 0:3, :], func=ACT.Copy, scale=SLOPE)
                banks[(c, j)] = vps
                smalls[(c, j)] = small

        def num_leaky(c):
            for j in range(CH // P):
                nc.vector.tensor_tensor(
                    out=by_runs_out(g_c[:, j * P : (j + 1) * P, 0:3]),
                    in0=by_runs_in(banks[(c, j)][:, 0:3, :]),
                    in1=by_runs_in(smalls[(c, j)][:]),
                    op=ALU.max,
                )

        def quantise_num(c):
            quantise(cf[:, 2, chunk(c)], sf[:, 2, chunk(c)], g_c[:])

        turn_tiles = {}
        frac_tiles = {}
        plane_tiles = {}
        grouped_a = {}

        def turns(c, s):
            turn = work.tile([P, CH], I32, tag="turn", bufs=4)
            nc.vector.tensor_scalar(
                out=turn[:], in0=xs[:, chunk(c)], scalar1=wq[:, s : s + 1], scalar2=bq[:, s : s + 1],
                op0=ALU.mult, op1=ALU.add,
            )
            turn_tiles[(c, s)] = turn

        def fracs(c, s):
            frac = work.tile([P, CH], F32, tag="frac", bufs=12)
            nc.vector.scalar_tensor_tensor(
                out=frac[:], in0=xs[:, chunk(c)], scalar=wq[:, s : s + 1], in1=turn_tiles[(c, s)][:],
                op0=ALU.mult, op1=ALU.subtract,
            )
            frac_tiles[(c, s)] = frac

        def sines(c, s):
            if s == 0:
                planes = work.tile([P, 4, CH], BF16, tag="planes")
                plane_tiles[c] = planes
            dst = plane_tiles[c][:, s, :] if s < 4 else g_bs[c][:, :, 0]
            nc.scalar.activation(
                out=dst, in_=frac_tiles[(c, s)][:], func=ACT.Sin, bias=sb[:, s : s + 1], scale=TWO_PI
            )

        slots = [(c, s) for c in range(NCH) for s in range(SLOTS)]
        done = []

        def sine_stream(steps):
            for step in range(steps):
                i = len(done)
                if i < len(slots):
                    turns(slots[i][0], slots[i][1])
                if 0 < i <= len(slots):
                    fracs(slots[i - 1][0], slots[i - 1][1])
                    sines(slots[i - 1][0], slots[i - 1][1])
                done.append(i)

        def group_sines(c, copy):
            g_a = work.tile([P, CH, 4], BF16, tag="g_a", align_bytes=64)
            regroup(copy, g_a[:], plane_tiles[c][:])
            grouped_a[c] = g_a

        biased = {}

        open_sums = {}

        def layer1_pass(c, i, m, cols, acc, start, stop):
            ms = slice(m * P, (m + 1) * P)
            nc.tensor.matmul_mx(
                out=acc[:],
                lhsT=cw[:, i, ms].bitcast(FP8X4), lhsT_scale=sw[:, i, ms],
                rhs=cf[:, i, cols].bitcast(FP8X4), rhs_scale=sf[:, i, cols],
                start=start, stop=stop,
            )

        def columns(c, half, width):
            lo = c * CH + half * HALF
            return slice(lo, lo + width * HALF)

        def layer1_open(c, half, width):
            cols = columns(c, half, width)
            for m in range(4):
                acc = psum.tile([P, width * HALF], F32, tag="bank")
                layer1_pass(c, 2, m, cols, acc, True, False)
                open_sums[(c, half, m)] = acc

        def layer1_more(c, half, width):
            cols = columns(c, half, width)
            for m in range(4):
                layer1_pass(c, 1, m, cols, open_sums[(c, half, m)], False, False)

        def layer1_close(c, half, width):
            cols = columns(c, half, width)
            pre1 = work.tile([P, 4, width * HALF], F32, tag="pre1", bufs=3)
            for m in range(4):
                acc = open_sums[(c, half, m)]
                layer1_pass(c, 0, m, cols, acc, False, True)
                nc.scalar.activation(out=pre1[:, m, :], in_=acc[:], func=ACT.Identity, bias=b1f[:, m : m + 1], scale=1.0)
            for w in range(width):
                biased[(c, half + w)] = pre1[:, :, w * HALF : (w + 1) * HALF]

        def quantise_and_layer1(c, width):
            layer1_open(c, 0, width)
            quantise(cf[:, 1, chunk(c)], sf[:, 1, chunk(c)], g_bs[c][:])
            layer1_more(c, 0, width)
            quantise(cf[:, 0, chunk(c)], sf[:, 0, chunk(c)], grouped_a[c][:])
            layer1_close(c, 0, width)
            if width == 1:
                layer1_open(c, 1, 1)
                layer1_more(c, 1, 1)
                layer1_close(c, 1, 1)

        grouped_h = {}
        hidden = {}

        def hidden_leaky(c, half):
            g_h = work.tile([P, HALF, 4], BF16, tag="g_h", bufs=4, align_bytes=64)
            grouped_h[(c, half)] = g_h
            v = biased[(c, half)].rearrange("p m n -> p n m")
            nc.vector.scalar_tensor_tensor(out=g_h[:], in0=v, scalar=SLOPE, in1=v, op0=ALU.mult, op1=ALU.max)

        def quantise_hidden(c, half):
            ch = work.tile([P, HALF], U32, tag="ch", bufs=4, align_bytes=64)
            sh = work.tile([P, HALF], U8, tag="sh", bufs=4, align_bytes=64)
            hidden[(c, half)] = (ch, sh)
            quantise(ch[:], sh[:], grouped_h[(c, half)][:])

        sums = {}
        pres = {}

        def layer2(c, half):
            ch, sh = hidden[(c, half)]
            for i in range(2):
                js = slice(i * P, (i + 1) * P)
                acc = psum.tile([P, H], F32, tag="bank")
                nc.tensor.matmul_mx(
                    out=acc[:],
                    lhsT=ch[:, js].bitcast(FP8X4), lhsT_scale=sh[:, js],
                    rhs=cw[:, 3, :].bitcast(FP8X4), rhs_scale=sw[:, 3, :],
                    start=True, stop=True,
                )
                sums[(c, 2 * half + i)] = acc

        def add_bias(c, j):
            pre = work.tile([P, H], F32, tag="pre", bufs=6)
            nc.vector.tensor_tensor(out=pre[:], in0=sums[(c, j)][:], in1=b2bc[:], op=ALU.add)
            pres[(c, j)] = pre

        def store(c, j, res):
            lo = c * CH + j * P
            nc.sync.dma_start(out=out[lo : lo + P, :], in_=res[:])

        def finish(c, j):
            res = work.tile([P, H], F32, tag="res", bufs=12)
            pre = pres[(c, j)]
            nc.vector.scalar_tensor_tensor(
                out=res[:], in0=pre[:], scalar=SLOPE, in1=pre[:], op0=ALU.mult, op1=ALU.max
            )
            store(c, j, res)

        def bias_columns():
            bps = psum.tile([P, 4, P], F32, tag="bank")
            for m in range(4):
                nc.tensor.transpose(out=bps[:, m, :], in_=b2bc[:, m * P : (m + 1) * P], identity=ident[:])
            nc.scalar.copy(out=b2c[:], in_=bps[:, :, 0])

        upright = {}
        turned = {}
        turned_lows = {}

        def turned_layer2(c, half):
            ch, sh = hidden[(c, half)]
            vt = work.tile([P, 4, HALF], F32, tag="vt")
            upright[(c, half)] = vt
            for pair in range(2):
                acc = psum.tile([P, 2, HALF], F32, tag="bank")
                for i in range(2):
                    m = 2 * pair + i
                    ms = slice(m * P, (m + 1) * P)
                    nc.tensor.matmul_mx(
                        out=acc[:, i, :],
                        lhsT=cw[:, 3, ms].bitcast(FP8X4), lhsT_scale=sw[:, 3, ms],
                        rhs=ch[:].bitcast(FP8X4), rhs_scale=sh[:],
                        start=True, stop=True,
                    )
                for i in range(2):
                    m = 2 * pair + i
                    nc.scalar.activation(
                        out=vt[:, m, :], in_=acc[:, i, :], func=ACT.Identity, bias=b2c[:, m : m + 1], scale=1.0
                    )

        def turn_back(c, half):
            for i in range(2):
                j = 2 * half + i
                tps = psum.tile([P, H], F32, tag="bank")
                for m in range(4):
                    nc.tensor.transpose(
                        out=tps[:, m * P : (m + 1) * P],
                        in_=upright[(c, half)][:, m, i * P : (i + 1) * P], identity=ident[:],
                    )
                turned[(c, j)] = tps
                tlow = work.tile([P, H], F32, tag="tlow", bufs=4)
                nc.scalar.activation(out=tlow[:], in_=tps[:], func=ACT.Copy, scale=SLOPE)
                turned_lows[(c, j)] = tlow

        def finish_turned(c, j):
            res = work.tile([P, H], F32, tag="res", bufs=12)
            nc.vector.tensor_tensor(out=res[:], in0=turned[(c, j)][:], in1=turned_lows[(c, j)][:], op=ALU.max)
            store(c, j, res)

        warm_up(16)
        regroup(nc.vector.tensor_copy, g_w1[:], w1s[:, 0:4, :])
        num_products(0)
        spread_points()
        num_products(1)
        num_leaky(0)
        quantise(cw[:, 0, :], sw[:, 0, :], g_w1[:])
        quantise_num(0)
        num_products(2)
        load_biases()
        nc.scalar.copy(out=g_wb[:, :, 0], in_=w1s[:, 4, :])
        num_leaky(1)
        constants()
        sine_stream(3)
        quantise_num(1)
        regroup(nc.scalar.copy, g_wc[:, :, 0:3], w1n[:])
        sine_stream(3)
        group_sines(0, nc.scalar.copy)
        num_leaky(2)
        quantise(cw[:, 1, :], sw[:, 1, :], g_wb[:])
        sine_stream(2)
        quantise_num(2)
        regroup(nc.scalar.copy, g_w2[:], w2[:])
        quantise(cw[:, 2, :], sw[:, 2, :], g_wc[:])
        spread_biases()
        quantise_and_layer1(0, 2)
        sine_stream(3)
        group_sines(1, nc.scalar.copy)
        bias_columns()
        quantise(cw[:, 3, :], sw[:, 3, :], g_w2[:])
        sine_stream(5)
        group_sines(2, nc.scalar.copy)
        hidden_leaky(0, 0)
        hidden_leaky(0, 1)
        quantise_hidden(0, 0)
        layer2(0, 0)
        quantise_hidden(0, 1)
        layer2(0, 1)
        quantise_and_layer1(1, 2)
        add_bias(0, 0)
        add_bias(0, 1)
        finish(0, 0)
        add_bias(0, 2)
        finish(0, 1)
        add_bias(0, 3)
        quantise_and_layer1(2, 1)
        finish(0, 2)
        finish(0, 3)
        hidden_leaky(1, 0)
        hidden_leaky(1, 1)
        quantise_hidden(1, 0)
        turned_layer2(1, 0)
        quantise_hidden(1, 1)
        turned_layer2(1, 1)
        hidden_leaky(2, 0)
        turn_back(1, 0)
        hidden_leaky(2, 1)
        turn_back(1, 1)
        quantise_hidden(2, 0)
        layer2(2, 0)
        quantise_hidden(2, 1)
        turned_layer2(2, 1)
        finish_turned(1, 0)
        finish_turned(1, 1)
        add_bias(2, 0)
        add_bias(2, 1)
        finish_turned(1, 2)
        finish_turned(1, 3)
        turn_back(2, 1)
        finish(2, 0)
        finish(2, 1)
        finish_turned(2, 2)
        finish_turned(2, 3)
